import numpy as np
import ml_dtypes


def mxq(x, axis, fmt="e4m3"):
    dtype, down = {"e4m3": (ml_dtypes.float8_e4m3fn, 7), "e5m2": (ml_dtypes.float8_e5m2, 14)}[fmt]
    v = np.moveaxis(np.asarray(x, np.float32).astype(ml_dtypes.bfloat16).astype(np.float64), axis, -1)
    blocks = v.reshape(v.shape[:-1] + (-1, 32))
    amax = np.abs(blocks).max(-1, keepdims=True)
    byte = np.maximum(np.where(amax > 0, np.frexp(amax)[1] - 1 + 127, 0) - down, 1)
    scale = np.exp2(byte - 127.0)
    codes = (blocks / scale).astype(np.float32).astype(dtype).astype(np.float64)
    return np.moveaxis((codes * scale).reshape(v.shape), -1, axis)


WIDE = False


def mx_kscale(k):
    if not WIDE:
        return np.ones(k)
    levels = np.array([10, -10, 5, -5, 0])
    a = np.random.permutation(np.resize(levels, k // 512 * 4)).reshape(k // 512, 4)
    idx = np.arange(k)
    return np.exp2(a[idx // 512, idx % 128 // 32])


BF16 = ml_dtypes.bfloat16


def bf(x):
    return np.asarray(x, np.float32).astype(BF16)


def f64(x):
    return np.asarray(x).astype(np.float64)


B, C_IN, C_OUT, N, T, K = 1, 512, 128, 1024, 3, 3


def cheb_laplacian(p):
    adj = 1.0 / (1.0 + np.exp(-p))
    adj = (adj + adj.T) * 0.5
    adj = adj * (1.0 - np.eye(N))
    deg = adj.sum(axis=1)
    dis = 1.0 / np.sqrt(deg)
    return -(dis[:, None] * adj * dis[None, :])


def setup_inputs():
    s = mx_kscale(C_IN)
    x = np.random.standard_normal((B, C_IN, 1, T)) + np.random.standard_normal((B, C_IN, N, T))
    tx1 = np.random.standard_normal((B, T, 1, C_IN)) + np.random.standard_normal((B, T, N, C_IN)) * 5.0 / np.sqrt(N)
    return {'x': bf(x * s[None, :, None, None]),
            'adj_param': bf(4.0 * np.random.standard_normal((N, N)) - 10.0 + 10.0 * np.eye(N)),
            'tx1': bf(tx1 * s),
            'cheb01': bf(np.random.standard_normal((B, T, N, C_OUT)) * 1.7),
            'w_cheb2': bf(np.random.standard_normal((C_IN, C_OUT)) / np.sqrt(C_IN) / s[:, None]),
            'cheb_bias': bf(np.random.standard_normal(C_OUT) * 0.3)}


def reference(x, adj_param, tx1, cheb01, w_cheb2, cheb_bias):
    s = cheb_laplacian(f64(adj_param))
    xt = f64(x).transpose(0, 3, 2, 1)
    tx2 = 2.0 * (mxq(s, 1, 'e4m3') @ mxq(f64(tx1), 2, 'e4m3')) - xt
    h = f64(cheb01) + (mxq(tx2, 3, 'e4m3') @ mxq(f64(w_cheb2), 0, 'e4m3'))
    h = h + f64(cheb_bias)
    return h.transpose(0, 3, 2, 1)

@@ -1,0 +1,259 @@
+from contextlib import ExitStack
+
+import concourse.mybir as mybir
+from concourse.masks import make_identity
+
+F32 = mybir.dt.float32
+BF16 = mybir.dt.bfloat16
+U32 = mybir.dt.uint32
+U8 = mybir.dt.uint8
+FP8X4 = mybir.dt.float8_e4m3fn_x4
+ALU = mybir.AluOpType
+ACT = mybir.ActivationFunctionType
+
+P = 128
+PACK = 4
+NODES = 1024
+C_IN = 512
+C_OUT = 128
+STEPS = 3
+ROWS = NODES // P
+PASSES = NODES // (P * PACK)
+HALF = 512
+HALVES = NODES // HALF
+PAIR = 2
+WIDE = PAIR * P
+
+FLOPS = 2 * STEPS * NODES * NODES * C_IN + 2 * STEPS * NODES * C_IN * C_OUT
+
+
+def tile_dynamicgraphspatialconv_pb_kernel(tc, x, adj_param, tx1, cheb01, w_cheb2, cheb_bias, out):
+    nc = tc.nc
+    with ExitStack() as ctx:
+        const = ctx.enter_context(tc.tile_pool(name="const", bufs=1))
+        keep = ctx.enter_context(tc.tile_pool(name="keep", bufs=1))
+        stage = ctx.enter_context(tc.tile_pool(name="stage", bufs=3))
+        banks = ctx.enter_context(tc.psum_pool(name="banks", bufs=4))
+        spread = ctx.enter_context(tc.psum_pool(name="spread", bufs=1))
+        results = ctx.enter_context(tc.psum_pool(name="results", bufs=2))
+
+        param = keep.tile([P, ROWS, NODES], BF16, tag="param_then_s")
+        param_rows = adj_param.rearrange("(b p) v -> p b v", p=P)
+        for b in range(ROWS):
+            nc.sync.dma_start(out=param[:, b, :], in_=param_rows[:, b, :])
+
+        w_raw = const.tile([P, PACK, C_OUT], BF16)
+        nc.sync.dma_start(out=w_raw[:], in_=w_cheb2.rearrange("(m p) o -> p m o", p=P))
+        bias_rows = const.tile([P, P], BF16)
+        nc.vector.memset(bias_rows[:], 0.0)
+        nc.sync.dma_start(out=bias_rows[0:1, :], in_=cheb_bias.rearrange("(r o) -> r o", r=1))
+
+        tx1_raw = keep.tile([P, STEPS, ROWS, C_IN], BF16)
+        cheb_raw = keep.tile([P, STEPS, ROWS, C_OUT], BF16)
+        x_sb = keep.tile([P, PACK, NODES, STEPS], BF16)
+        nc.sync.dma_start(out=tx1_raw[:, 0], in_=tx1[0, 0].rearrange("(b p) c -> p b c", p=P))
+        for t in range(STEPS):
+            nc.sync.dma_start(out=cheb_raw[:, t], in_=cheb01[0, t].rearrange("(b p) o -> p b o", p=P))
+        for m in range(PACK):
+            nc.sync.dma_start(out=x_sb[:, m], in_=x[0, m * P : (m + 1) * P])
+        for t in range(1, STEPS):
+            nc.sync.dma_start(out=tx1_raw[:, t], in_=tx1[0, t].rearrange("(b p) c -> p b c", p=P))
+
+        ident_f = const.tile([P, P], F32)
+        make_identity(nc, ident_f[:])
+        ident_b = const.tile([P, P], BF16)
+        make_identity(nc, ident_b[:])
+        off_diag = const.tile([P, P], F32)
+        nc.vector.tensor_scalar(
+            out=off_diag[:], in0=ident_f[:], scalar1=-1.0, scalar2=1.0, op0=ALU.mult, op1=ALU.add
+        )
+
+        w_grouped = const.tile([P, C_OUT, PACK], BF16, align_bytes=64)
+        nc.vector.tensor_copy(out=w_grouped[:], in_=w_raw[:].rearrange("p m o -> p o m"))
+        w_codes = const.tile([P, C_OUT], U32, align_bytes=64)
+        w_scales = const.tile([P, C_OUT], U8, align_bytes=64)
+        nc.vector.quantize_mx(
+            out=w_codes[:].bitcast(FP8X4), scales=w_scales[:], in_=w_grouped[:].rearrange("p o m -> p (o m)")
+        )
+
+        bias_turned = banks.tile([P, P], BF16, tag="bank")
+        nc.tensor.transpose(out=bias_turned[:], in_=bias_rows[:], identity=ident_b[:])
+        bias_col = const.tile([P, 1], F32)
+        nc.vector.tensor_copy(out=bias_col[:], in_=bias_turned[:, 0:1])
+
+        sig = keep.tile([P, ROWS, NODES], F32)
+        both = keep.tile([P, ROWS, NODES], F32)
+        row_sums = const.tile([P, HALVES, ROWS], F32)
+
+        def sigmoid_piece(b, h):
+            cols = slice(h * HALF, (h + 1) * HALF)
+            nc.scalar.activation(out=sig[:, b, cols], in_=param[:, b, cols], func=ACT.Sigmoid)
+            if b // PACK == h:
+                diag = slice(b * P, (b + 1) * P)
+                nc.gpsimd.tensor_tensor(out=sig[:, b, diag], in0=sig[:, b, diag], in1=off_diag[:], op=ALU.mult)
+
+        def symmetrise(b, h):
+            cols = slice(h * HALF, (h + 1) * HALF)
+            turned = banks.tile([P, PACK, P], F32, tag="bank")
+            for i in range(PACK):
+                nc.tensor.transpose(
+                    out=turned[:, i, :], in_=sig[:, PACK * h + i, b * P : (b + 1) * P], identity=ident_f[:]
+                )
+            nc.vector.scalar_tensor_tensor(
+                out=both[:, b, cols],
+                in0=turned[:].rearrange("p i w -> p (i w)"),
+                scalar=1.0,
+                in1=sig[:, b, cols],
+                op0=ALU.mult,
+                op1=ALU.add,
+                accum_out=row_sums[:, h, b : b + 1],
+            )
+
+        top = range(0, PACK)
+        bottom = range(PACK, ROWS)
+        for b in top:
+            sigmoid_piece(b, 0)
+        for b in top:
+            symmetrise(b, 0)
+        for b in bottom:
+            sigmoid_piece(b, 1)
+        for b in bottom:
+            symmetrise(b, 1)
+        for b in top:
+            sigmoid_piece(b, 1)
+        for b in bottom:
+            sigmoid_piece(b, 0)
+            symmetrise(b, 0)
+        for b in top:
+            symmetrise(b, 1)
+        table_warm = const.tile([P, 1], F32)
+        nc.scalar.activation(out=table_warm[:], in_=sig[:, ROWS - 1, 0:1], func=ACT.Sqrt)
+
+        tx1_codes = keep.tile([P, STEPS, PASSES, C_IN], U32, align_bytes=64)
+        tx1_scales = keep.tile([P, STEPS, PASSES, C_IN], U8, align_bytes=64)
+
+        def quantise_tx1(t):
+            for g in range(PASSES):
+                tx1_grouped = stage.tile([P, C_IN, PACK], BF16, align_bytes=64)
+                nc.scalar.copy(
+                    out=tx1_grouped[:], in_=tx1_raw[:, t, g * PACK : (g + 1) * PACK, :].rearrange("p j c -> p c j")
+                )
+                nc.vector.quantize_mx(
+                    out=tx1_codes[:, t, g, :].bitcast(FP8X4),
+                    scales=tx1_scales[:, t, g, :],
+                    in_=tx1_grouped[:].rearrange("p c j -> p (c j)"),
+                )
+
+        quantise_tx1(0)
+
+        cheb_t = keep.tile([P, STEPS, NODES], BF16)
+        for t in range(STEPS):
+            cheb_turned = banks.tile([P, ROWS, P], BF16, tag="bank")
+            for b in range(ROWS):
+                nc.tensor.transpose(out=cheb_turned[:, b, :], in_=cheb_raw[:, t, b, :], identity=ident_b[:])
+            nc.scalar.copy(out=cheb_t[:, t, :], in_=cheb_turned[:].rearrange("p b w -> p (b w)"))
+
+        deg2 = const.tile([P, ROWS], F32)
+        nc.vector.tensor_tensor(out=deg2[:], in0=row_sums[:, 0, :], in1=row_sums[:, 1, :], op=ALU.add)
+        root = const.tile([P, ROWS], F32)
+        nc.scalar.activation(out=root[:], in_=deg2[:], func=ACT.Sqrt)
+        rnorm = const.tile([P, ROWS], F32)
+        nc.vector.reciprocal(out=rnorm[:], in_=root[:])
+        rnorm_neg = const.tile([P, ROWS], F32)
+        nc.vector.tensor_scalar(out=rnorm_neg[:], in0=rnorm[:], scalar1=-1.0, scalar2=None, op0=ALU.mult)
+        repeated = const.tile([P, ROWS, P], F32)
+        nc.vector.tensor_copy(out=repeated[:], in_=rnorm[:].unsqueeze(2).to_broadcast([P, ROWS, P]))
+        rnorm_cols = []
+        for h in range(HALVES):
+            rnorm_half = spread.tile([P, PACK, P], F32, name="rnorm_half%d" % h)
+            for i in range(PACK):
+                nc.tensor.transpose(out=rnorm_half[:, i, :], in_=repeated[:, PACK * h + i, :], identity=ident_f[:])
+            rnorm_cols.append(rnorm_half)
+
+        s_bf = keep.tile([P, ROWS, NODES], BF16, tag="param_then_s")
+        s_codes = keep.tile([P, NODES // WIDE, PASSES, WIDE], U32, align_bytes=64)
+        s_scales = keep.tile([P, NODES // WIDE, PASSES, WIDE], U8, align_bytes=64)
+        for h in range(HALVES):
+            cols = slice(h * HALF, (h + 1) * HALF)
+            for b in range(ROWS):
+                nc.vector.scalar_tensor_tensor(
+                    out=s_bf[:, b, cols],
+                    in0=both[:, b, cols],
+                    scalar=rnorm_neg[:, b : b + 1],
+                    in1=rnorm_cols[h][:].rearrange("p i w -> p (i w)"),
+                    op0=ALU.mult,
+                    op1=ALU.mult,
+                )
+            for q in range(h * HALF // WIDE, (h + 1) * HALF // WIDE):
+                s_grouped = stage.tile([P, PASSES, WIDE, PACK], BF16, align_bytes=64)
+                for g in range(PASSES):
+                    nc.scalar.copy(
+                        out=s_grouped[:, g],
+                        in_=s_bf[:, g * PACK : (g + 1) * PACK, q * WIDE : (q + 1) * WIDE].rearrange("p j v -> p v j"),
+                    )
+                nc.vector.quantize_mx(
+                    out=s_codes[:, q].rearrange("p g v -> p (g v)").bitcast(FP8X4),
+                    scales=s_scales[:, q].rearrange("p g v -> p (g v)"),
+                    in_=s_grouped[:].rearrange("p g v j -> p (g v j)"),
+                )
+
+        for t in range(1, STEPS):
+            quantise_tx1(t)
+
+        tx2_codes = keep.tile([P, STEPS, NODES], U32, align_bytes=64)
+        tx2_scales = keep.tile([P, STEPS, NODES], U8, align_bytes=64)
+        for t in range(STEPS):
+            for q in range(NODES // WIDE):
+                tx2_grouped = stage.tile([P, PAIR, P, PACK], BF16, align_bytes=64)
+                for k in range(PAIR):
+                    nodes = slice(q * WIDE + k * P, q * WIDE + (k + 1) * P)
+                    acc = banks.tile([P, PACK, P], F32, tag="bank")
+                    for m in range(PACK):
+                        for g in range(PASSES):
+                            nc.tensor.matmul_mx(
+                                out=acc[:, m, :],
+                                lhsT=tx1_codes[:, t, g, m * P : (m + 1) * P].bitcast(FP8X4),
+                                lhsT_scale=tx1_scales[:, t, g, m * P : (m + 1) * P],
+                                rhs=s_codes[:, q, g, k * P : (k + 1) * P].bitcast(FP8X4),
+                                rhs_scale=s_scales[:, q, g, k * P : (k + 1) * P],
+                                start=(g == 0),
+                                stop=(g == PASSES - 1),
+                            )
+                    nc.vector.scalar_tensor_tensor(
+                        out=tx2_grouped[:, k],
+                        in0=acc[:].rearrange("p m v -> p v m"),
+                        scalar=2.0,
+                        in1=x_sb[:, :, nodes, t].rearrange("p m v -> p v m"),
+                        op0=ALU.mult,
+                        op1=ALU.subtract,
+                    )
+                wide = slice(q * WIDE, (q + 1) * WIDE)
+                nc.vector.quantize_mx(
+                    out=tx2_codes[:, t, wide].bitcast(FP8X4),
+                    scales=tx2_scales[:, t, wide],
+                    in_=tx2_grouped[:].rearrange("p k v m -> p (k v m)"),
+                )
+                if t == STEPS - 1:
+                    for k in range(PAIR):
+                        nodes = slice(q * WIDE + k * P, q * WIDE + (k + 1) * P)
+                        mixed = results.tile([P, STEPS, P], F32)
+                        for u in range(STEPS):
+                            nc.tensor.matmul_mx(
+                                out=mixed[:, u, :],
+                                lhsT=w_codes[:].bitcast(FP8X4),
+                                lhsT_scale=w_scales[:],
+                                rhs=tx2_codes[:, u, nodes].bitcast(FP8X4),
+                                rhs_scale=tx2_scales[:, u, nodes],
+                                start=True,
+                                stop=True,
+                            )
+                        answer = stage.tile([P, P, STEPS], F32)
+                        nc.vector.scalar_tensor_tensor(
+                            out=answer[:],
+                            in0=mixed[:].rearrange("p u v -> p v u"),
+                            scalar=bias_col[:, 0:1],
+                            in1=cheb_t[:, :, nodes].rearrange("p u v -> p v u"),
+                            op0=ALU.add,
+                            op1=ALU.add,
+                        )
+                        nc.sync.dma_start(out=out[0, :, nodes, :], in_=answer[:])

@@ -21,39 +21,48 @@ ROWS = NODES // P
 PASSES = NODES // (P * PACK)
 HALF = 512
 HALVES = NODES // HALF
-PAIR = 2
-WIDE = PAIR * P
+TILES = NODES // P
+ITEMS = STEPS * TILES
+RUN = 4
+AHEAD = 3
 
 FLOPS = 2 * STEPS * NODES * NODES * C_IN + 2 * STEPS * NODES * C_IN * C_OUT
+
+
+def grouped_view(dst):
+    return dst.rearrange("p (c i) j -> p c j i", i=RUN)
+
+
+def rows_view(src):
+    return src.rearrange("p j (c i) -> p c j i", i=RUN)
 
 
 def tile_dynamicgraphspatialconv_pb_kernel(tc, x, adj_param, tx1, cheb01, w_cheb2, cheb_bias, out):
     nc = tc.nc
     with ExitStack() as ctx:
+        ctx.enter_context(tc.manual_schedule())
         const = ctx.enter_context(tc.tile_pool(name="const", bufs=1))
         keep = ctx.enter_context(tc.tile_pool(name="keep", bufs=1))
         stage = ctx.enter_context(tc.tile_pool(name="stage", bufs=3))
-        banks = ctx.enter_context(tc.psum_pool(name="banks", bufs=4))
-        spread = ctx.enter_context(tc.psum_pool(name="spread", bufs=1))
+        banks = ctx.enter_context(tc.psum_pool(name="banks", bufs=6))
         results = ctx.enter_context(tc.psum_pool(name="results", bufs=2))
 
-        param = keep.tile([P, ROWS, NODES], BF16, tag="param_then_s")
+        bias_rows = const.tile([P, P], BF16)
+        nc.vector.memset(bias_rows[:], 0.0)
+
+        param = keep.tile([P, ROWS, NODES], BF16)
         param_rows = adj_param.rearrange("(b p) v -> p b v", p=P)
         for b in range(ROWS):
             nc.sync.dma_start(out=param[:, b, :], in_=param_rows[:, b, :])
-
+        tx1_raw = keep.tile([P, STEPS, ROWS, C_IN], BF16)
+        nc.sync.dma_start(out=tx1_raw[:, 0], in_=tx1[0, 0].rearrange("(b p) c -> p b c", p=P))
         w_raw = const.tile([P, PACK, C_OUT], BF16)
         nc.sync.dma_start(out=w_raw[:], in_=w_cheb2.rearrange("(m p) o -> p m o", p=P))
-        bias_rows = const.tile([P, P], BF16)
-        nc.vector.memset(bias_rows[:], 0.0)
         nc.sync.dma_start(out=bias_rows[0:1, :], in_=cheb_bias.rearrange("(r o) -> r o", r=1))
-
-        tx1_raw = keep.tile([P, STEPS, ROWS, C_IN], BF16)
         cheb_raw = keep.tile([P, STEPS, ROWS, C_OUT], BF16)
-        x_sb = keep.tile([P, PACK, NODES, STEPS], BF16)
-        nc.sync.dma_start(out=tx1_raw[:, 0], in_=tx1[0, 0].rearrange("(b p) c -> p b c", p=P))
         for t in range(STEPS):
             nc.sync.dma_start(out=cheb_raw[:, t], in_=cheb01[0, t].rearrange("(b p) o -> p b o", p=P))
+        x_sb = keep.tile([P, PACK, NODES, STEPS], BF16)
         for m in range(PACK):
             nc.sync.dma_start(out=x_sb[:, m], in_=x[0, m * P : (m + 1) * P])
         for t in range(1, STEPS):
@@ -67,19 +76,6 @@ def tile_dynamicgraphspatialconv_pb_kernel(tc, x, adj_param, tx1, cheb01, w_cheb
         nc.vector.tensor_scalar(
             out=off_diag[:], in0=ident_f[:], scalar1=-1.0, scalar2=1.0, op0=ALU.mult, op1=ALU.add
         )
-
-        w_grouped = const.tile([P, C_OUT, PACK], BF16, align_bytes=64)
-        nc.vector.tensor_copy(out=w_grouped[:], in_=w_raw[:].rearrange("p m o -> p o m"))
-        w_codes = const.tile([P, C_OUT], U32, align_bytes=64)
-        w_scales = const.tile([P, C_OUT], U8, align_bytes=64)
-        nc.vector.quantize_mx(
-            out=w_codes[:].bitcast(FP8X4), scales=w_scales[:], in_=w_grouped[:].rearrange("p o m -> p (o m)")
-        )
-
-        bias_turned = banks.tile([P, P], BF16, tag="bank")
-        nc.tensor.transpose(out=bias_turned[:], in_=bias_rows[:], identity=ident_b[:])
-        bias_col = const.tile([P, 1], F32)
-        nc.vector.tensor_copy(out=bias_col[:], in_=bias_turned[:, 0:1])
 
         sig = keep.tile([P, ROWS, NODES], F32)
         both = keep.tile([P, ROWS, NODES], F32)
@@ -109,6 +105,22 @@ def tile_dynamicgraphspatialconv_pb_kernel(tc, x, adj_param, tx1, cheb01, w_cheb
                 accum_out=row_sums[:, h, b : b + 1],
             )
 
+        tx1_codes = keep.tile([P, STEPS, PASSES, C_IN], U32, align_bytes=64)
+        tx1_scales = keep.tile([P, STEPS, PASSES, C_IN], U8, align_bytes=64)
+        tx1_grouped = {}
+
+        def tx1_rows(t, g):
+            tx1_grouped[(t, g)] = stage.tile([P, C_IN, PACK], BF16, align_bytes=64, name="tx1_grouped")
+            return rows_view(tx1_raw[:, t, g * PACK : (g + 1) * PACK, :])
+
+        def quantise_tx1(t):
+            for g in range(PASSES):
+                nc.vector.quantize_mx(
+                    out=tx1_codes[:, t, g, :].bitcast(FP8X4),
+                    scales=tx1_scales[:, t, g, :],
+                    in_=tx1_grouped[(t, g)][:].rearrange("p c j -> p (c j)"),
+                )
+
         top = range(0, PACK)
         bottom = range(PACK, ROWS)
         for b in top:
@@ -119,6 +131,10 @@ def tile_dynamicgraphspatialconv_pb_kernel(tc, x, adj_param, tx1, cheb01, w_cheb
             sigmoid_piece(b, 1)
         for b in bottom:
             symmetrise(b, 1)
+        rows = tx1_rows(0, 0)
+        nc.gpsimd.tensor_scalar(
+            out=grouped_view(tx1_grouped[(0, 0)][:]), in0=rows, scalar1=1.0, scalar2=0.0, op0=ALU.mult, op1=ALU.add
+        )
         for b in top:
             sigmoid_piece(b, 1)
         for b in bottom:
@@ -126,134 +142,155 @@ def tile_dynamicgraphspatialconv_pb_kernel(tc, x, adj_param, tx1, cheb01, w_cheb
             symmetrise(b, 0)
         for b in top:
             symmetrise(b, 1)
+        rows = tx1_rows(0, 1)
+        nc.scalar.copy(out=grouped_view(tx1_grouped[(0, 1)][:]), in_=rows)
         table_warm = const.tile([P, 1], F32)
         nc.scalar.activation(out=table_warm[:], in_=sig[:, ROWS - 1, 0:1], func=ACT.Sqrt)
 
-        tx1_codes = keep.tile([P, STEPS, PASSES, C_IN], U32, align_bytes=64)
-        tx1_scales = keep.tile([P, STEPS, PASSES, C_IN], U8, align_bytes=64)
-
-        def quantise_tx1(t):
-            for g in range(PASSES):
-                tx1_grouped = stage.tile([P, C_IN, PACK], BF16, align_bytes=64)
-                nc.scalar.copy(
-                    out=tx1_grouped[:], in_=tx1_raw[:, t, g * PACK : (g + 1) * PACK, :].rearrange("p j c -> p c j")
-                )
-                nc.vector.quantize_mx(
-                    out=tx1_codes[:, t, g, :].bitcast(FP8X4),
-                    scales=tx1_scales[:, t, g, :],
-                    in_=tx1_grouped[:].rearrange("p c j -> p (c j)"),
-                )
-
-        quantise_tx1(0)
-
-        cheb_t = keep.tile([P, STEPS, NODES], BF16)
-        for t in range(STEPS):
-            cheb_turned = banks.tile([P, ROWS, P], BF16, tag="bank")
-            for b in range(ROWS):
-                nc.tensor.transpose(out=cheb_turned[:, b, :], in_=cheb_raw[:, t, b, :], identity=ident_b[:])
-            nc.scalar.copy(out=cheb_t[:, t, :], in_=cheb_turned[:].rearrange("p b w -> p (b w)"))
+        bias_turned = banks.tile([P, P], BF16, tag="bank")
+        nc.tensor.transpose(out=bias_turned[:], in_=bias_rows[:], identity=ident_b[:])
 
         deg2 = const.tile([P, ROWS], F32)
         nc.vector.tensor_tensor(out=deg2[:], in0=row_sums[:, 0, :], in1=row_sums[:, 1, :], op=ALU.add)
         root = const.tile([P, ROWS], F32)
         nc.scalar.activation(out=root[:], in_=deg2[:], func=ACT.Sqrt)
+        w_grouped = const.tile([P, C_OUT, PACK], BF16, align_bytes=64)
+        nc.vector.tensor_copy(out=w_grouped[:], in_=w_raw[:].rearrange("p m o -> p o m"))
         rnorm = const.tile([P, ROWS], F32)
         nc.vector.reciprocal(out=rnorm[:], in_=root[:])
-        rnorm_neg = const.tile([P, ROWS], F32)
-        nc.vector.tensor_scalar(out=rnorm_neg[:], in0=rnorm[:], scalar1=-1.0, scalar2=None, op0=ALU.mult)
-        repeated = const.tile([P, ROWS, P], F32)
-        nc.vector.tensor_copy(out=repeated[:], in_=rnorm[:].unsqueeze(2).to_broadcast([P, ROWS, P]))
-        rnorm_cols = []
-        for h in range(HALVES):
-            rnorm_half = spread.tile([P, PACK, P], F32, name="rnorm_half%d" % h)
-            for i in range(PACK):
-                nc.tensor.transpose(out=rnorm_half[:, i, :], in_=repeated[:, PACK * h + i, :], identity=ident_f[:])
-            rnorm_cols.append(rnorm_half)
+        bias_col = const.tile([P, 1], F32)
+        nc.vector.tensor_copy(out=bias_col[:], in_=bias_turned[:, 0:1])
+        w_codes = const.tile([P, C_OUT], U32, align_bytes=64)
+        w_scales = const.tile([P, C_OUT], U8, align_bytes=64)
+        nc.vector.quantize_mx(
+            out=w_codes[:].bitcast(FP8X4), scales=w_scales[:], in_=w_grouped[:].rearrange("p o m -> p (o m)")
+        )
+        quantise_tx1(0)
 
-        s_bf = keep.tile([P, ROWS, NODES], BF16, tag="param_then_s")
-        s_codes = keep.tile([P, NODES // WIDE, PASSES, WIDE], U32, align_bytes=64)
-        s_scales = keep.tile([P, NODES // WIDE, PASSES, WIDE], U8, align_bytes=64)
-        for h in range(HALVES):
-            cols = slice(h * HALF, (h + 1) * HALF)
+        s_codes = keep.tile([P, TILES, PASSES, P], U32, align_bytes=64)
+        s_scales = keep.tile([P, TILES, PASSES, P], U8, align_bytes=64)
+        tx2_codes = keep.tile([P, STEPS, NODES], U32, align_bytes=64)
+        tx2_scales = keep.tile([P, STEPS, NODES], U8, align_bytes=64)
+        cheb_t = keep.tile([P, STEPS, NODES], BF16)
+        s_grouped = {}
+        acc = {}
+        tx2_grouped = {}
+
+        cheb_turned = {}
+
+        def turn_cheb(t):
+            cheb_turned[t] = banks.tile([P, ROWS, P], BF16, tag="bank", name="cheb_turned")
             for b in range(ROWS):
+                nc.tensor.transpose(out=cheb_turned[t][:, b, :], in_=cheb_raw[:, t, b, :], identity=ident_b[:])
+
+        def keep_cheb(t):
+            nc.scalar.copy(out=cheb_t[:, t, :], in_=cheb_turned[t][:].rearrange("p b w -> p (b w)"))
+
+        def make_s(r):
+            scaled = stage.tile([P, NODES], F32)
+            nc.scalar.activation(out=scaled[:], in_=both[:, r, :], func=ACT.Copy, scale=rnorm[:, r : r + 1])
+            s_grouped[r] = stage.tile([P, PASSES, P, PACK], BF16, align_bytes=64, name="s_grouped")
+            for g in range(PASSES):
+                turned = banks.tile([P, PACK, P], F32, tag="bank")
+                for j in range(PACK):
+                    b = g * PACK + j
+                    nc.tensor.transpose(out=turned[:, j, :], in_=scaled[:, b * P : (b + 1) * P], identity=ident_f[:])
                 nc.vector.scalar_tensor_tensor(
-                    out=s_bf[:, b, cols],
-                    in0=both[:, b, cols],
-                    scalar=rnorm_neg[:, b : b + 1],
-                    in1=rnorm_cols[h][:].rearrange("p i w -> p (i w)"),
+                    out=s_grouped[r][:, g],
+                    in0=turned[:].rearrange("p j v -> p v j"),
+                    scalar=-1.0,
+                    in1=rnorm[:, g * PACK : (g + 1) * PACK].unsqueeze(1).to_broadcast([P, P, PACK]),
                     op0=ALU.mult,
                     op1=ALU.mult,
                 )
-            for q in range(h * HALF // WIDE, (h + 1) * HALF // WIDE):
-                s_grouped = stage.tile([P, PASSES, WIDE, PACK], BF16, align_bytes=64)
+
+        def quantise_s(r):
+            nc.vector.quantize_mx(
+                out=s_codes[:, r].rearrange("p g v -> p (g v)").bitcast(FP8X4),
+                scales=s_scales[:, r].rearrange("p g v -> p (g v)"),
+                in_=s_grouped[r][:].rearrange("p g v j -> p (g v j)"),
+            )
+
+        def first_product(t, r):
+            acc[(t, r)] = banks.tile([P, PACK, P], F32, tag="bank", name="acc")
+            for m in range(PACK):
                 for g in range(PASSES):
-                    nc.scalar.copy(
-                        out=s_grouped[:, g],
-                        in_=s_bf[:, g * PACK : (g + 1) * PACK, q * WIDE : (q + 1) * WIDE].rearrange("p j v -> p v j"),
+                    nc.tensor.matmul_mx(
+                        out=acc[(t, r)][:, m, :],
+                        lhsT=tx1_codes[:, t, g, m * P : (m + 1) * P].bitcast(FP8X4),
+                        lhsT_scale=tx1_scales[:, t, g, m * P : (m + 1) * P],
+                        rhs=s_codes[:, r, g, :].bitcast(FP8X4),
+                        rhs_scale=s_scales[:, r, g, :],
+                        start=(g == 0),
+                        stop=(g == PASSES - 1),
                     )
-                nc.vector.quantize_mx(
-                    out=s_codes[:, q].rearrange("p g v -> p (g v)").bitcast(FP8X4),
-                    scales=s_scales[:, q].rearrange("p g v -> p (g v)"),
-                    in_=s_grouped[:].rearrange("p g v j -> p (g v j)"),
-                )
 
-        for t in range(1, STEPS):
-            quantise_tx1(t)
+        def subtract_x(t, r):
+            tx2_grouped[(t, r)] = stage.tile([P, P, PACK], BF16, align_bytes=64, name="tx2_grouped")
+            nc.vector.scalar_tensor_tensor(
+                out=tx2_grouped[(t, r)][:],
+                in0=acc[(t, r)][:].rearrange("p m v -> p v m"),
+                scalar=2.0,
+                in1=x_sb[:, :, r * P : (r + 1) * P, t].rearrange("p m v -> p v m"),
+                op0=ALU.mult,
+                op1=ALU.subtract,
+            )
 
-        tx2_codes = keep.tile([P, STEPS, NODES], U32, align_bytes=64)
-        tx2_scales = keep.tile([P, STEPS, NODES], U8, align_bytes=64)
-        for t in range(STEPS):
-            for q in range(NODES // WIDE):
-                tx2_grouped = stage.tile([P, PAIR, P, PACK], BF16, align_bytes=64)
-                for k in range(PAIR):
-                    nodes = slice(q * WIDE + k * P, q * WIDE + (k + 1) * P)
-                    acc = banks.tile([P, PACK, P], F32, tag="bank")
-                    for m in range(PACK):
-                        for g in range(PASSES):
-                            nc.tensor.matmul_mx(
-                                out=acc[:, m, :],
-                                lhsT=tx1_codes[:, t, g, m * P : (m + 1) * P].bitcast(FP8X4),
-                                lhsT_scale=tx1_scales[:, t, g, m * P : (m + 1) * P],
-                                rhs=s_codes[:, q, g, k * P : (k + 1) * P].bitcast(FP8X4),
-                                rhs_scale=s_scales[:, q, g, k * P : (k + 1) * P],
-                                start=(g == 0),
-                                stop=(g == PASSES - 1),
-                            )
-                    nc.vector.scalar_tensor_tensor(
-                        out=tx2_grouped[:, k],
-                        in0=acc[:].rearrange("p m v -> p v m"),
-                        scalar=2.0,
-                        in1=x_sb[:, :, nodes, t].rearrange("p m v -> p v m"),
-                        op0=ALU.mult,
-                        op1=ALU.subtract,
-                    )
-                wide = slice(q * WIDE, (q + 1) * WIDE)
-                nc.vector.quantize_mx(
-                    out=tx2_codes[:, t, wide].bitcast(FP8X4),
-                    scales=tx2_scales[:, t, wide],
-                    in_=tx2_grouped[:].rearrange("p k v m -> p (k v m)"),
+        def quantise_tx2(t, r):
+            nc.vector.quantize_mx(
+                out=tx2_codes[:, t, r * P : (r + 1) * P].bitcast(FP8X4),
+                scales=tx2_scales[:, t, r * P : (r + 1) * P],
+                in_=tx2_grouped[(t, r)][:].rearrange("p v m -> p (v m)"),
+            )
+
+        def finish(r):
+            nodes = slice(r * P, (r + 1) * P)
+            mixed = results.tile([P, STEPS, P], F32)
+            for u in range(STEPS):
+                nc.tensor.matmul_mx(
+                    out=mixed[:, u, :],
+                    lhsT=w_codes[:].bitcast(FP8X4),
+                    lhsT_scale=w_scales[:],
+                    rhs=tx2_codes[:, u, nodes].bitcast(FP8X4),
+                    rhs_scale=tx2_scales[:, u, nodes],
+                    start=True,
+                    stop=True,
                 )
-                if t == STEPS - 1:
-                    for k in range(PAIR):
-                        nodes = slice(q * WIDE + k * P, q * WIDE + (k + 1) * P)
-                        mixed = results.tile([P, STEPS, P], F32)
-                        for u in range(STEPS):
-                            nc.tensor.matmul_mx(
-                                out=mixed[:, u, :],
-                                lhsT=w_codes[:].bitcast(FP8X4),
-                                lhsT_scale=w_scales[:],
-                                rhs=tx2_codes[:, u, nodes].bitcast(FP8X4),
-                                rhs_scale=tx2_scales[:, u, nodes],
-                                start=True,
-                                stop=True,
-                            )
-                        answer = stage.tile([P, P, STEPS], F32)
-                        nc.vector.scalar_tensor_tensor(
-                            out=answer[:],
-                            in0=mixed[:].rearrange("p u v -> p v u"),
-                            scalar=bias_col[:, 0:1],
-                            in1=cheb_t[:, :, nodes].rearrange("p u v -> p v u"),
-                            op0=ALU.add,
-                            op1=ALU.add,
-                        )
-                        nc.sync.dma_start(out=out[0, :, nodes, :], in_=answer[:])
+            answer = stage.tile([P, P, STEPS], F32)
+            nc.vector.scalar_tensor_tensor(
+                out=answer[:],
+                in0=mixed[:].rearrange("p u v -> p v u"),
+                scalar=bias_col[:, 0:1],
+                in1=cheb_t[:, :, nodes].rearrange("p u v -> p v u"),
+                op0=ALU.add,
+                op1=ALU.add,
+            )
+            nc.sync.dma_start(out=out[0, :, nodes, :], in_=answer[:])
+
+        for i in range(ITEMS + 5):
+            if i < ITEMS:
+                t, r = divmod(i, TILES)
+                if r == 0:
+                    turn_cheb(t)
+                if t == 0:
+                    make_s(r)
+                if r == 0:
+                    keep_cheb(t)
+                if t + 1 < STEPS and r % 2 == 1 and r // 2 < PASSES:
+                    rows = tx1_rows(t + 1, r // 2)
+                    nc.scalar.copy(out=grouped_view(tx1_grouped[(t + 1, r // 2)][:]), in_=rows)
+                if t + 1 < STEPS and r == TILES - AHEAD:
+                    quantise_tx1(t + 1)
+            if 0 <= i - 1 < TILES:
+                quantise_s(i - 1)
+            if 0 <= i - 2 < ITEMS:
+                t, r = divmod(i - 2, TILES)
+                first_product(t, r)
+            if 0 <= i - 3 < ITEMS:
+                t, r = divmod(i - 3, TILES)
+                subtract_x(t, r)
+            if 0 <= i - 4 < ITEMS:
+                t, r = divmod(i - 4, TILES)
+                quantise_tx2(t, r)
+            if ITEMS - TILES <= i - 5 < ITEMS:
+                finish(i - 5 - (ITEMS - TILES))

@@ -44,6 +44,7 @@ def tile_dynamicgraphspatialconv_pb_kernel(tc, x, adj_param, tx1, cheb01, w_cheb
         const = ctx.enter_context(tc.tile_pool(name="const", bufs=1))
         keep = ctx.enter_context(tc.tile_pool(name="keep", bufs=1))
         stage = ctx.enter_context(tc.tile_pool(name="stage", bufs=3))
+        early = ctx.enter_context(tc.tile_pool(name="early", bufs=(STEPS - 1) * PASSES))
         banks = ctx.enter_context(tc.psum_pool(name="banks", bufs=6))
         results = ctx.enter_context(tc.psum_pool(name="results", bufs=2))
 
@@ -55,7 +56,8 @@ def tile_dynamicgraphspatialconv_pb_kernel(tc, x, adj_param, tx1, cheb01, w_cheb
         for b in range(ROWS):
             nc.sync.dma_start(out=param[:, b, :], in_=param_rows[:, b, :])
         tx1_raw = keep.tile([P, STEPS, ROWS, C_IN], BF16)
-        nc.sync.dma_start(out=tx1_raw[:, 0], in_=tx1[0, 0].rearrange("(b p) c -> p b c", p=P))
+        for t in range(STEPS - 1):
+            nc.sync.dma_start(out=tx1_raw[:, t], in_=tx1[0, t].rearrange("(b p) c -> p b c", p=P))
         w_raw = const.tile([P, PACK, C_OUT], BF16)
         nc.sync.dma_start(out=w_raw[:], in_=w_cheb2.rearrange("(m p) o -> p m o", p=P))
         nc.sync.dma_start(out=bias_rows[0:1, :], in_=cheb_bias.rearrange("(r o) -> r o", r=1))
@@ -65,8 +67,8 @@ def tile_dynamicgraphspatialconv_pb_kernel(tc, x, adj_param, tx1, cheb01, w_cheb
         x_sb = keep.tile([P, PACK, NODES, STEPS], BF16)
         for m in range(PACK):
             nc.sync.dma_start(out=x_sb[:, m], in_=x[0, m * P : (m + 1) * P])
-        for t in range(1, STEPS):
-            nc.sync.dma_start(out=tx1_raw[:, t], in_=tx1[0, t].rearrange("(b p) c -> p b c", p=P))
+        last = STEPS - 1
+        nc.sync.dma_start(out=tx1_raw[:, last], in_=tx1[0, last].rearrange("(b p) c -> p b c", p=P))
 
         ident_f = const.tile([P, P], F32)
         make_identity(nc, ident_f[:])
@@ -110,7 +112,7 @@ def tile_dynamicgraphspatialconv_pb_kernel(tc, x, adj_param, tx1, cheb01, w_cheb
         tx1_grouped = {}
 
         def tx1_rows(t, g):
-            tx1_grouped[(t, g)] = stage.tile([P, C_IN, PACK], BF16, align_bytes=64, name="tx1_grouped")
+            tx1_grouped[(t, g)] = early.tile([P, C_IN, PACK], BF16, align_bytes=64, name="tx1_grouped")
             return rows_view(tx1_raw[:, t, g * PACK : (g + 1) * PACK, :])
 
         def quantise_tx1(t):
@@ -131,10 +133,11 @@ def tile_dynamicgraphspatialconv_pb_kernel(tc, x, adj_param, tx1, cheb01, w_cheb
             sigmoid_piece(b, 1)
         for b in bottom:
             symmetrise(b, 1)
-        rows = tx1_rows(0, 0)
-        nc.gpsimd.tensor_scalar(
-            out=grouped_view(tx1_grouped[(0, 0)][:]), in0=rows, scalar1=1.0, scalar2=0.0, op0=ALU.mult, op1=ALU.add
-        )
+        for t in range(STEPS - 1):
+            rows = tx1_rows(t, 0)
+            nc.gpsimd.tensor_scalar(
+                out=grouped_view(tx1_grouped[(t, 0)][:]), in0=rows, scalar1=1.0, scalar2=0.0, op0=ALU.mult, op1=ALU.add
+            )
         for b in top:
             sigmoid_piece(b, 1)
         for b in bottom:
@@ -142,8 +145,9 @@ def tile_dynamicgraphspatialconv_pb_kernel(tc, x, adj_param, tx1, cheb01, w_cheb
             symmetrise(b, 0)
         for b in top:
             symmetrise(b, 1)
-        rows = tx1_rows(0, 1)
-        nc.scalar.copy(out=grouped_view(tx1_grouped[(0, 1)][:]), in_=rows)
+        for t in range(STEPS - 1):
+            rows = tx1_rows(t, 1)
+            nc.scalar.copy(out=grouped_view(tx1_grouped[(t, 1)][:]), in_=rows)
         table_warm = const.tile([P, 1], F32)
         nc.scalar.activation(out=table_warm[:], in_=sig[:, ROWS - 1, 0:1], func=ACT.Sqrt)
 
@@ -256,14 +260,13 @@ def tile_dynamicgraphspatialconv_pb_kernel(tc, x, adj_param, tx1, cheb01, w_cheb
                     start=True,
                     stop=True,
                 )
+            biased = stage.tile([P, P, STEPS], F32)
+            nc.scalar.activation(
+                out=biased[:], in_=mixed[:].rearrange("p u v -> p v u"), func=ACT.Identity, bias=bias_col[:, 0:1]
+            )
             answer = stage.tile([P, P, STEPS], F32)
-            nc.vector.scalar_tensor_tensor(
-                out=answer[:],
-                in0=mixed[:].rearrange("p u v -> p v u"),
-                scalar=bias_col[:, 0:1],
-                in1=cheb_t[:, :, nodes].rearrange("p u v -> p v u"),
-                op0=ALU.add,
-                op1=ALU.add,
+            nc.gpsimd.tensor_tensor(
+                out=answer[:], in0=biased[:], in1=cheb_t[:, :, nodes].rearrange("p u v -> p v u"), op=ALU.add
             )
             nc.sync.dma_start(out=out[0, :, nodes, :], in_=answer[:])
 
@@ -276,9 +279,9 @@ def tile_dynamicgraphspatialconv_pb_kernel(tc, x, adj_param, tx1, cheb01, w_cheb
                     make_s(r)
                 if r == 0:
                     keep_cheb(t)
-                if t + 1 < STEPS and r % 2 == 1 and r // 2 < PASSES:
-                    rows = tx1_rows(t + 1, r // 2)
-                    nc.scalar.copy(out=grouped_view(tx1_grouped[(t + 1, r // 2)][:]), in_=rows)
+                if t + 1 == last and r < PASSES:
+                    rows = tx1_rows(last, r)
+                    nc.scalar.copy(out=grouped_view(tx1_grouped[(last, r)][:]), in_=rows)
                 if t + 1 < STEPS and r == TILES - AHEAD:
                     quantise_tx1(t + 1)
             if 0 <= i - 1 < TILES:

@@ -56,17 +56,23 @@ def tile_dynamicgraphspatialconv_pb_kernel(tc, x, adj_param, tx1, cheb01, w_cheb
         for b in range(ROWS):
             nc.sync.dma_start(out=param[:, b, :], in_=param_rows[:, b, :])
         tx1_raw = keep.tile([P, STEPS, ROWS, C_IN], BF16)
-        for t in range(STEPS - 1):
-            nc.sync.dma_start(out=tx1_raw[:, t], in_=tx1[0, t].rearrange("(b p) c -> p b c", p=P))
+        nc.sync.dma_start(out=tx1_raw[:, 0], in_=tx1[0, 0].rearrange("(b p) c -> p b c", p=P))
         w_raw = const.tile([P, PACK, C_OUT], BF16)
         nc.sync.dma_start(out=w_raw[:], in_=w_cheb2.rearrange("(m p) o -> p m o", p=P))
         nc.sync.dma_start(out=bias_rows[0:1, :], in_=cheb_bias.rearrange("(r o) -> r o", r=1))
+        x_sb = keep.tile([P, PACK, NODES, STEPS], BF16)
+        x_rows = x[0].rearrange("(m p) v t -> p m v t", p=P)
+
+        def load_x(first, end):
+            nc.sync.dma_start(out=x_sb[:, :, first:end, :], in_=x_rows[:, :, first:end, :])
+
+        load_x(0, 256)
+        nc.sync.dma_start(out=tx1_raw[:, 1], in_=tx1[0, 1].rearrange("(b p) c -> p b c", p=P))
+        load_x(256, 512)
+        load_x(512, NODES)
         cheb_raw = keep.tile([P, STEPS, ROWS, C_OUT], BF16)
         for t in range(STEPS):
-            nc.sync.dma_start(out=cheb_raw[:, t], in_=cheb01[0, t].rearrange("(b p) o -> p b o", p=P))
-        x_sb = keep.tile([P, PACK, NODES, STEPS], BF16)
-        for m in range(PACK):
-            nc.sync.dma_start(out=x_sb[:, m], in_=x[0, m * P : (m + 1) * P])
+            nc.sync.dma_start(out=cheb_raw[:, t], in_=cheb01[0, t].rearrange("(p b) o -> p b o", p=P))
         last = STEPS - 1
         nc.sync.dma_start(out=tx1_raw[:, last], in_=tx1[0, last].rearrange("(b p) c -> p b c", p=P))
 
@@ -188,7 +194,9 @@ def tile_dynamicgraphspatialconv_pb_kernel(tc, x, adj_param, tx1, cheb01, w_cheb
                 nc.tensor.transpose(out=cheb_turned[t][:, b, :], in_=cheb_raw[:, t, b, :], identity=ident_b[:])
 
         def keep_cheb(t):
-            nc.scalar.copy(out=cheb_t[:, t, :], in_=cheb_turned[t][:].rearrange("p b w -> p (b w)"))
+            nc.scalar.copy(
+                out=cheb_t[:, t, :].rearrange("p (w b) -> p w b", b=ROWS), in_=cheb_turned[t][:].rearrange("p b w -> p w b")
+            )
 
         def make_s(r):
             scaled = stage.tile([P, NODES], F32)
@@ -273,12 +281,12 @@ def tile_dynamicgraphspatialconv_pb_kernel(tc, x, adj_param, tx1, cheb01, w_cheb
         for i in range(ITEMS + 5):
             if i < ITEMS:
                 t, r = divmod(i, TILES)
-                if r == 0:
-                    turn_cheb(t)
+                if t == 1 and r < STEPS:
+                    turn_cheb(r)
                 if t == 0:
                     make_s(r)
-                if r == 0:
-                    keep_cheb(t)
+                if t == 1 and r < STEPS:
+                    keep_cheb(r)
                 if t + 1 == last and r < PASSES:
                     rows = tx1_rows(last, r)
                     nc.scalar.copy(out=grouped_view(tx1_grouped[(last, r)][:]), in_=rows)

@@ -22,9 +22,10 @@ PASSES = NODES // (P * PACK)
 HALF = 512
 HALVES = NODES // HALF
 TILES = NODES // P
-ITEMS = STEPS * TILES
 RUN = 4
-AHEAD = 3
+QUARTERS = 4
+LAGS = (1, 2, 4)
+ORDER = (1, 0, 2)
 
 FLOPS = 2 * STEPS * NODES * NODES * C_IN + 2 * STEPS * NODES * C_IN * C_OUT
 
@@ -44,9 +45,10 @@ def tile_dynamicgraphspatialconv_pb_kernel(tc, x, adj_param, tx1, cheb01, w_cheb
         const = ctx.enter_context(tc.tile_pool(name="const", bufs=1))
         keep = ctx.enter_context(tc.tile_pool(name="keep", bufs=1))
         stage = ctx.enter_context(tc.tile_pool(name="stage", bufs=3))
-        early = ctx.enter_context(tc.tile_pool(name="early", bufs=(STEPS - 1) * PASSES))
-        banks = ctx.enter_context(tc.psum_pool(name="banks", bufs=6))
+        early = ctx.enter_context(tc.tile_pool(name="early", bufs=5))
+        banks = ctx.enter_context(tc.psum_pool(name="banks", bufs=4))
         results = ctx.enter_context(tc.psum_pool(name="results", bufs=2))
+        factors = ctx.enter_context(tc.psum_pool(name="factors", bufs=2))
 
         bias_rows = const.tile([P, P], BF16)
         nc.vector.memset(bias_rows[:], 0.0)
@@ -56,25 +58,28 @@ def tile_dynamicgraphspatialconv_pb_kernel(tc, x, adj_param, tx1, cheb01, w_cheb
         for b in range(ROWS):
             nc.sync.dma_start(out=param[:, b, :], in_=param_rows[:, b, :])
         tx1_raw = keep.tile([P, STEPS, ROWS, C_IN], BF16)
-        nc.sync.dma_start(out=tx1_raw[:, 0], in_=tx1[0, 0].rearrange("(b p) c -> p b c", p=P))
-        w_raw = const.tile([P, PACK, C_OUT], BF16)
-        nc.sync.dma_start(out=w_raw[:], in_=w_cheb2.rearrange("(m p) o -> p m o", p=P))
-        nc.sync.dma_start(out=bias_rows[0:1, :], in_=cheb_bias.rearrange("(r o) -> r o", r=1))
+
+        def load_tx1(t):
+            nc.sync.dma_start(out=tx1_raw[:, t], in_=tx1[0, t].rearrange("(b p) c -> p b c", p=P))
+
         x_sb = keep.tile([P, PACK, NODES, STEPS], BF16)
         x_rows = x[0].rearrange("(m p) v t -> p m v t", p=P)
 
         def load_x(first, end):
             nc.sync.dma_start(out=x_sb[:, :, first:end, :], in_=x_rows[:, :, first:end, :])
 
+        load_tx1(0)
+        w_raw = const.tile([P, PACK, C_OUT], BF16)
+        nc.sync.dma_start(out=w_raw[:], in_=w_cheb2.rearrange("(m p) o -> p m o", p=P))
+        nc.sync.dma_start(out=bias_rows[0:1, :], in_=cheb_bias.rearrange("(r o) -> r o", r=1))
+        load_tx1(1)
         load_x(0, 256)
-        nc.sync.dma_start(out=tx1_raw[:, 1], in_=tx1[0, 1].rearrange("(b p) c -> p b c", p=P))
+        load_tx1(2)
         load_x(256, 512)
         load_x(512, NODES)
         cheb_raw = keep.tile([P, STEPS, ROWS, C_OUT], BF16)
         for t in range(STEPS):
             nc.sync.dma_start(out=cheb_raw[:, t], in_=cheb01[0, t].rearrange("(p b) o -> p b o", p=P))
-        last = STEPS - 1
-        nc.sync.dma_start(out=tx1_raw[:, last], in_=tx1[0, last].rearrange("(b p) c -> p b c", p=P))
 
         ident_f = const.tile([P, P], F32)
         make_identity(nc, ident_f[:])
@@ -87,134 +92,164 @@ def tile_dynamicgraphspatialconv_pb_kernel(tc, x, adj_param, tx1, cheb01, w_cheb
 
         sig = keep.tile([P, ROWS, NODES], F32)
         both = keep.tile([P, ROWS, NODES], F32)
-        row_sums = const.tile([P, HALVES, ROWS], F32)
+        row_sums = const.tile([P, ROWS, QUARTERS], F32)
+        nc.vector.memset(row_sums[:], 0.0)
 
-        def sigmoid_piece(b, h):
-            cols = slice(h * HALF, (h + 1) * HALF)
+        def sigmoid_piece(b, first, count):
+            cols = slice(first * P, (first + count) * P)
             nc.scalar.activation(out=sig[:, b, cols], in_=param[:, b, cols], func=ACT.Sigmoid)
-            if b // PACK == h:
+            if first <= b < first + count:
                 diag = slice(b * P, (b + 1) * P)
                 nc.gpsimd.tensor_tensor(out=sig[:, b, diag], in0=sig[:, b, diag], in1=off_diag[:], op=ALU.mult)
 
-        def symmetrise(b, h):
-            cols = slice(h * HALF, (h + 1) * HALF)
+        def symmetrise(b, first, count):
+            cols = slice(first * P, (first + count) * P)
             turned = banks.tile([P, PACK, P], F32, tag="bank")
-            for i in range(PACK):
+            for i in range(count):
                 nc.tensor.transpose(
-                    out=turned[:, i, :], in_=sig[:, PACK * h + i, b * P : (b + 1) * P], identity=ident_f[:]
+                    out=turned[:, i, :], in_=sig[:, first + i, b * P : (b + 1) * P], identity=ident_f[:]
                 )
+            slot = first * QUARTERS // ROWS
             nc.vector.scalar_tensor_tensor(
                 out=both[:, b, cols],
-                in0=turned[:].rearrange("p i w -> p (i w)"),
-                scalar=1.0,
+                in0=turned[:, 0:count, :].rearrange("p i w -> p (i w)"),
+                scalar=-1.0,
                 in1=sig[:, b, cols],
                 op0=ALU.mult,
-                op1=ALU.add,
-                accum_out=row_sums[:, h, b : b + 1],
+                op1=ALU.subtract,
+                accum_out=row_sums[:, b, slot : slot + 1],
             )
 
         tx1_codes = keep.tile([P, STEPS, PASSES, C_IN], U32, align_bytes=64)
         tx1_scales = keep.tile([P, STEPS, PASSES, C_IN], U8, align_bytes=64)
         tx1_grouped = {}
 
-        def tx1_rows(t, g):
-            tx1_grouped[(t, g)] = early.tile([P, C_IN, PACK], BF16, align_bytes=64, name="tx1_grouped")
-            return rows_view(tx1_raw[:, t, g * PACK : (g + 1) * PACK, :])
+        def regroup_views(t, g, first, end):
+            if (t, g) not in tx1_grouped:
+                tx1_grouped[(t, g)] = early.tile([P, C_IN, PACK], BF16, align_bytes=64, name="tx1_grouped")
+            return (
+                grouped_view(tx1_grouped[(t, g)][:, first:end, :]),
+                rows_view(tx1_raw[:, t, g * PACK : (g + 1) * PACK, first:end]),
+            )
 
-        def quantise_tx1(t):
-            for g in range(PASSES):
-                nc.vector.quantize_mx(
-                    out=tx1_codes[:, t, g, :].bitcast(FP8X4),
-                    scales=tx1_scales[:, t, g, :],
-                    in_=tx1_grouped[(t, g)][:].rearrange("p c j -> p (c j)"),
-                )
+        def regroup_on_gpsimd(t, g):
+            for first in range(0, C_IN, P):
+                dst, rows = regroup_views(t, g, first, first + P)
+                nc.gpsimd.tensor_scalar(out=dst, in0=rows, scalar1=1.0, scalar2=0.0, op0=ALU.mult, op1=ALU.add)
+
+        def regroup_on_scalar(t, g, half):
+            dst, rows = regroup_views(t, g, half * C_IN // 2, (half + 1) * C_IN // 2)
+            nc.scalar.copy(out=dst, in_=rows)
+
+        def quantise_tx1(t, g):
+            nc.vector.quantize_mx(
+                out=tx1_codes[:, t, g, :].bitcast(FP8X4),
+                scales=tx1_scales[:, t, g, :],
+                in_=tx1_grouped[(t, g)][:].rearrange("p c j -> p (c j)"),
+            )
 
         top = range(0, PACK)
         bottom = range(PACK, ROWS)
-        for b in top:
-            sigmoid_piece(b, 0)
-        for b in top:
-            symmetrise(b, 0)
+        for first in (0, 2):
+            for b in (0, 1):
+                sigmoid_piece(b, first, 2)
+        for b in (2, 3):
+            sigmoid_piece(b, 0, 4)
+        for first in (0, 2):
+            for b in top:
+                symmetrise(b, first, 2)
         for b in bottom:
-            sigmoid_piece(b, 1)
+            sigmoid_piece(b, 4, 4)
         for b in bottom:
-            symmetrise(b, 1)
-        for t in range(STEPS - 1):
-            rows = tx1_rows(t, 0)
-            nc.gpsimd.tensor_scalar(
-                out=grouped_view(tx1_grouped[(t, 0)][:]), in0=rows, scalar1=1.0, scalar2=0.0, op0=ALU.mult, op1=ALU.add
-            )
+            symmetrise(b, 4, 4)
+        regroup_on_gpsimd(0, 0)
+        regroup_on_gpsimd(1, 0)
+        regroup_on_gpsimd(1, 1)
+        regroup_on_gpsimd(2, 1)
         for b in top:
-            sigmoid_piece(b, 1)
+            sigmoid_piece(b, 4, 4)
         for b in bottom:
-            sigmoid_piece(b, 0)
-            symmetrise(b, 0)
-        for b in top:
-            symmetrise(b, 1)
-        for t in range(STEPS - 1):
-            rows = tx1_rows(t, 1)
-            nc.scalar.copy(out=grouped_view(tx1_grouped[(t, 1)][:]), in_=rows)
+            sigmoid_piece(b, 0, 4)
+        for first in (4, 6):
+            for b in (first, first + 1):
+                symmetrise(b, 0, 4)
+            for b in top:
+                symmetrise(b, first, 2)
         table_warm = const.tile([P, 1], F32)
         nc.scalar.activation(out=table_warm[:], in_=sig[:, ROWS - 1, 0:1], func=ACT.Sqrt)
+        regroup_on_scalar(0, 1, 0)
+        regroup_on_scalar(0, 1, 1)
 
         bias_turned = banks.tile([P, P], BF16, tag="bank")
         nc.tensor.transpose(out=bias_turned[:], in_=bias_rows[:], identity=ident_b[:])
 
         deg2 = const.tile([P, ROWS], F32)
-        nc.vector.tensor_tensor(out=deg2[:], in0=row_sums[:, 0, :], in1=row_sums[:, 1, :], op=ALU.add)
+        nc.vector.tensor_reduce(out=deg2[:], in_=row_sums[:], axis=mybir.AxisListType.X, op=ALU.add)
         root = const.tile([P, ROWS], F32)
-        nc.scalar.activation(out=root[:], in_=deg2[:], func=ACT.Sqrt)
-        w_grouped = const.tile([P, C_OUT, PACK], BF16, align_bytes=64)
-        nc.vector.tensor_copy(out=w_grouped[:], in_=w_raw[:].rearrange("p m o -> p o m"))
+        nc.scalar.activation(out=root[:], in_=deg2[:], func=ACT.Sqrt, scale=-1.0)
         rnorm = const.tile([P, ROWS], F32)
         nc.vector.reciprocal(out=rnorm[:], in_=root[:])
-        bias_col = const.tile([P, 1], F32)
-        nc.vector.tensor_copy(out=bias_col[:], in_=bias_turned[:, 0:1])
+        quantise_tx1(0, 0)
+        w_grouped = const.tile([P, C_OUT, PACK], BF16, align_bytes=64)
         w_codes = const.tile([P, C_OUT], U32, align_bytes=64)
         w_scales = const.tile([P, C_OUT], U8, align_bytes=64)
-        nc.vector.quantize_mx(
-            out=w_codes[:].bitcast(FP8X4), scales=w_scales[:], in_=w_grouped[:].rearrange("p o m -> p (o m)")
-        )
-        quantise_tx1(0)
+        bias_col = const.tile([P, 1], F32)
+
+        def group_w():
+            nc.vector.tensor_copy(out=w_grouped[:], in_=w_raw[:].rearrange("p m o -> p o m"))
+
+        def quantise_w():
+            nc.vector.quantize_mx(
+                out=w_codes[:].bitcast(FP8X4), scales=w_scales[:], in_=w_grouped[:].rearrange("p o m -> p (o m)")
+            )
+            nc.vector.tensor_copy(out=bias_col[:], in_=bias_turned[:, 0:1])
+
+        factor = []
+        for half in range(HALVES):
+            factor.append(factors.tile([P, PACK, P], F32, name="factor"))
+            for i in range(PACK):
+                r = half * PACK + i
+                nc.tensor.transpose(
+                    out=factor[half][:, i, :], in_=rnorm[:, r : r + 1].to_broadcast([P, P]), identity=ident_f[:]
+                )
 
         s_codes = keep.tile([P, TILES, PASSES, P], U32, align_bytes=64)
         s_scales = keep.tile([P, TILES, PASSES, P], U8, align_bytes=64)
         tx2_codes = keep.tile([P, STEPS, NODES], U32, align_bytes=64)
         tx2_scales = keep.tile([P, STEPS, NODES], U8, align_bytes=64)
         cheb_t = keep.tile([P, STEPS, NODES], BF16)
+        scaled = {}
         s_grouped = {}
         acc = {}
         tx2_grouped = {}
 
-        cheb_turned = {}
-
         def turn_cheb(t):
-            cheb_turned[t] = banks.tile([P, ROWS, P], BF16, tag="bank", name="cheb_turned")
+            turned = banks.tile([P, ROWS, P], BF16, tag="bank", name="cheb_turned")
             for b in range(ROWS):
-                nc.tensor.transpose(out=cheb_turned[t][:, b, :], in_=cheb_raw[:, t, b, :], identity=ident_b[:])
-
-        def keep_cheb(t):
+                nc.tensor.transpose(out=turned[:, b, :], in_=cheb_raw[:, t, b, :], identity=ident_b[:])
             nc.scalar.copy(
-                out=cheb_t[:, t, :].rearrange("p (w b) -> p w b", b=ROWS), in_=cheb_turned[t][:].rearrange("p b w -> p w b")
+                out=cheb_t[:, t, :].rearrange("p (w b) -> p w b", b=ROWS), in_=turned[:].rearrange("p b w -> p w b")
             )
 
-        def make_s(r):
-            scaled = stage.tile([P, NODES], F32)
-            nc.scalar.activation(out=scaled[:], in_=both[:, r, :], func=ACT.Copy, scale=rnorm[:, r : r + 1])
-            s_grouped[r] = stage.tile([P, PASSES, P, PACK], BF16, align_bytes=64, name="s_grouped")
-            for g in range(PASSES):
-                turned = banks.tile([P, PACK, P], F32, tag="bank")
-                for j in range(PACK):
-                    b = g * PACK + j
-                    nc.tensor.transpose(out=turned[:, j, :], in_=scaled[:, b * P : (b + 1) * P], identity=ident_f[:])
-                nc.vector.scalar_tensor_tensor(
-                    out=s_grouped[r][:, g],
-                    in0=turned[:].rearrange("p j v -> p v j"),
-                    scalar=-1.0,
-                    in1=rnorm[:, g * PACK : (g + 1) * PACK].unsqueeze(1).to_broadcast([P, P, PACK]),
-                    op0=ALU.mult,
-                    op1=ALU.mult,
+        def scale_rows(r):
+            scaled[r] = stage.tile([P, ROWS, P], F32, name="scaled")
+            for b in range(ROWS):
+                nc.scalar.activation(
+                    out=scaled[r][:, b, :], in_=both[:, b, r * P : (r + 1) * P], func=ACT.Copy, scale=rnorm[:, b : b + 1]
                 )
+
+        def scale_columns(r, g):
+            if g == 0:
+                s_grouped[r] = stage.tile([P, PASSES, P, PACK], BF16, align_bytes=64, name="s_grouped")
+            nc.vector.tensor_tensor(
+                out=grouped_view(s_grouped[r][:, g]),
+                in0=rows_view(scaled[r][:, g * PACK : (g + 1) * PACK, :]),
+                in1=factor[r // PACK][:, r % PACK, :]
+                .rearrange("p (c i) -> p c i", i=RUN)
+                .unsqueeze(2)
+                .to_broadcast([P, P // RUN, PACK, RUN]),
+                op=ALU.mult,
+            )
 
         def quantise_s(r):
             nc.vector.quantize_mx(
@@ -268,40 +303,67 @@ def tile_dynamicgraphspatialconv_pb_kernel(tc, x, adj_param, tx1, cheb01, w_cheb
                     start=True,
                     stop=True,
                 )
+            answer = stage.tile([P, P, STEPS], F32)
+            if r == TILES - 1:
+                nc.vector.scalar_tensor_tensor(
+                    out=answer[:],
+                    in0=mixed[:].rearrange("p u v -> p v u"),
+                    scalar=bias_col[:, 0:1],
+                    in1=cheb_t[:, :, nodes].rearrange("p u v -> p v u"),
+                    op0=ALU.add,
+                    op1=ALU.add,
+                )
+                nc.sync.dma_start(out=out[0, :, nodes, :], in_=answer[:])
+                return
             biased = stage.tile([P, P, STEPS], F32)
             nc.scalar.activation(
                 out=biased[:], in_=mixed[:].rearrange("p u v -> p v u"), func=ACT.Identity, bias=bias_col[:, 0:1]
             )
-            answer = stage.tile([P, P, STEPS], F32)
             nc.gpsimd.tensor_tensor(
                 out=answer[:], in0=biased[:], in1=cheb_t[:, :, nodes].rearrange("p u v -> p v u"), op=ALU.add
             )
             nc.sync.dma_start(out=out[0, :, nodes, :], in_=answer[:])
 
-        for i in range(ITEMS + 5):
-            if i < ITEMS:
-                t, r = divmod(i, TILES)
-                if t == 1 and r < STEPS:
-                    turn_cheb(r)
-                if t == 0:
-                    make_s(r)
-                if t == 1 and r < STEPS:
-                    keep_cheb(r)
-                if t + 1 == last and r < PASSES:
-                    rows = tx1_rows(last, r)
-                    nc.scalar.copy(out=grouped_view(tx1_grouped[(last, r)][:]), in_=rows)
-                if t + 1 < STEPS and r == TILES - AHEAD:
-                    quantise_tx1(t + 1)
-            if 0 <= i - 1 < TILES:
-                quantise_s(i - 1)
-            if 0 <= i - 2 < ITEMS:
-                t, r = divmod(i - 2, TILES)
-                first_product(t, r)
-            if 0 <= i - 3 < ITEMS:
-                t, r = divmod(i - 3, TILES)
-                subtract_x(t, r)
-            if 0 <= i - 4 < ITEMS:
-                t, r = divmod(i - 4, TILES)
+        waiting = []
+
+        def quantise_one():
+            if waiting:
+                t, r = waiting.pop(0)
                 quantise_tx2(t, r)
-            if ITEMS - TILES <= i - 5 < ITEMS:
-                finish(i - 5 - (ITEMS - TILES))
+                if t == last:
+                    finish(r)
+
+        last = STEPS - 1
+        scale_rows(0)
+        scale_rows(1)
+        for k in range(TILES + LAGS[last]):
+            items = [(t, k - LAGS[t]) for t in ORDER if 0 <= k - LAGS[t] < TILES]
+            if k + 2 < TILES:
+                if k < 2:
+                    regroup_on_scalar(last, 0, k)
+                scale_rows(k + 2)
+            for item in items:
+                first_product(*item)
+            extra = []
+            if k < TILES:
+                scale_columns(k, 0)
+                extra = [lambda: scale_columns(k, 1), lambda: quantise_s(k)]
+            if k == 0:
+                quantise_tx1(0, 1)
+                extra.insert(1, group_w)
+            if k == 1:
+                quantise_w()
+            for n, item in enumerate(items):
+                subtract_x(*item)
+                quantise_one()
+                waiting.append(item)
+                if extra:
+                    extra.pop(0)()
+            for step in extra:
+                step()
+            if k + 1 in LAGS[1:]:
+                for g in range(PASSES):
+                    quantise_tx1(LAGS.index(k + 1), g)
+            if 0 <= LAGS[last] - k < STEPS:
+                turn_cheb(LAGS[last] - k)
+        quantise_one()

@@ -45,6 +45,8 @@ def tile_dynamicgraphspatialconv_pb_kernel(tc, x, adj_param, tx1, cheb01, w_cheb
         const = ctx.enter_context(tc.tile_pool(name="const", bufs=1))
         keep = ctx.enter_context(tc.tile_pool(name="keep", bufs=1))
         stage = ctx.enter_context(tc.tile_pool(name="stage", bufs=3))
+        leave = ctx.enter_context(tc.tile_pool(name="leave", bufs=2))
+        ahead = ctx.enter_context(tc.tile_pool(name="ahead", bufs=6))
         early = ctx.enter_context(tc.tile_pool(name="early", bufs=5))
         banks = ctx.enter_context(tc.psum_pool(name="banks", bufs=4))
         results = ctx.enter_context(tc.psum_pool(name="results", bufs=2))
@@ -272,13 +274,21 @@ def tile_dynamicgraphspatialconv_pb_kernel(tc, x, adj_param, tx1, cheb01, w_cheb
                         stop=(g == PASSES - 1),
                     )
 
+        x_words = {}
+
+        def lay_x(t, r):
+            x_words[(t, r)] = ahead.tile([P, P, PACK], BF16, name="x_words")
+            nc.scalar.copy(
+                out=grouped_view(x_words[(t, r)][:]), in_=rows_view(x_sb[:, :, r * P : (r + 1) * P, t])
+            )
+
         def subtract_x(t, r):
             tx2_grouped[(t, r)] = stage.tile([P, P, PACK], BF16, align_bytes=64, name="tx2_grouped")
             nc.vector.scalar_tensor_tensor(
                 out=tx2_grouped[(t, r)][:],
                 in0=acc[(t, r)][:].rearrange("p m v -> p v m"),
                 scalar=2.0,
-                in1=x_sb[:, :, r * P : (r + 1) * P, t].rearrange("p m v -> p v m"),
+                in1=x_words[(t, r)][:],
                 op0=ALU.mult,
                 op1=ALU.subtract,
             )
@@ -303,7 +313,7 @@ def tile_dynamicgraphspatialconv_pb_kernel(tc, x, adj_param, tx1, cheb01, w_cheb
                     start=True,
                     stop=True,
                 )
-            answer = stage.tile([P, P, STEPS], F32)
+            answer = leave.tile([P, P, STEPS], F32)
             if r == TILES - 1:
                 nc.vector.scalar_tensor_tensor(
                     out=answer[:],
@@ -315,7 +325,7 @@ def tile_dynamicgraphspatialconv_pb_kernel(tc, x, adj_param, tx1, cheb01, w_cheb
                 )
                 nc.sync.dma_start(out=out[0, :, nodes, :], in_=answer[:])
                 return
-            biased = stage.tile([P, P, STEPS], F32)
+            biased = leave.tile([P, P, STEPS], F32)
             nc.scalar.activation(
                 out=biased[:], in_=mixed[:].rearrange("p u v -> p v u"), func=ACT.Identity, bias=bias_col[:, 0:1]
             )
@@ -333,11 +343,14 @@ def tile_dynamicgraphspatialconv_pb_kernel(tc, x, adj_param, tx1, cheb01, w_cheb
                 if t == last:
                     finish(r)
 
+        def slot_items(k):
+            return [(t, k - LAGS[t]) for t in ORDER if 0 <= k - LAGS[t] < TILES]
+
         last = STEPS - 1
         scale_rows(0)
         scale_rows(1)
         for k in range(TILES + LAGS[last]):
-            items = [(t, k - LAGS[t]) for t in ORDER if 0 <= k - LAGS[t] < TILES]
+            items = slot_items(k)
             if k + 2 < TILES:
                 if k < 2:
                     regroup_on_scalar(last, 0, k)
@@ -364,6 +377,8 @@ def tile_dynamicgraphspatialconv_pb_kernel(tc, x, adj_param, tx1, cheb01, w_cheb
             if k + 1 in LAGS[1:]:
                 for g in range(PASSES):
                     quantise_tx1(LAGS.index(k + 1), g)
+            for item in slot_items(k + 1):
+                lay_x(*item)
             if 0 <= LAGS[last] - k < STEPS:
                 turn_cheb(LAGS[last] - k)
         quantise_one()

@@ -22,7 +22,12 @@ PASSES = NODES // (P * PACK)
 HALF = 512
 HALVES = NODES // HALF
 TILES = NODES // P
+EARLY = 2
 RUN = 4
+GREG = ((0, 0), (0, 1), (1, 0), (1, 1))
+HEADLAY = ((0, "scalar"),)
+SPLAN = {-1: (("s", 0), ("s", 1)), 0: (("l", 1), ("s", 2)), 1: (("t", 2, 0, 0), ("t", 2, 0, 1), ("s", 3)), 2: (("t", 2, 1, 0), ("t", 2, 1, 1), ("s", 4)), 3: (("s", 5), ("l", 4)), 4: (("s", 6),), 5: (("s", 7), ("l", 7))}
+GLAY = {0: (2, 3), 2: (5,), 3: (6,)}
 QUARTERS = 4
 LAGS = (1, 2, 4)
 ORDER = (1, 0, 2)
@@ -45,8 +50,8 @@ def tile_dynamicgraphspatialconv_pb_kernel(tc, x, adj_param, tx1, cheb01, w_cheb
         const = ctx.enter_context(tc.tile_pool(name="const", bufs=1))
         keep = ctx.enter_context(tc.tile_pool(name="keep", bufs=1))
         stage = ctx.enter_context(tc.tile_pool(name="stage", bufs=3))
-        leave = ctx.enter_context(tc.tile_pool(name="leave", bufs=2))
-        ahead = ctx.enter_context(tc.tile_pool(name="ahead", bufs=6))
+        leave = ctx.enter_context(tc.tile_pool(name="leave", bufs=4))
+        shared = ctx.enter_context(tc.tile_pool(name="shared", bufs=1))
         early = ctx.enter_context(tc.tile_pool(name="early", bufs=5))
         banks = ctx.enter_context(tc.psum_pool(name="banks", bufs=4))
         results = ctx.enter_context(tc.psum_pool(name="results", bufs=2))
@@ -55,7 +60,7 @@ def tile_dynamicgraphspatialconv_pb_kernel(tc, x, adj_param, tx1, cheb01, w_cheb
         bias_rows = const.tile([P, P], BF16)
         nc.vector.memset(bias_rows[:], 0.0)
 
-        param = keep.tile([P, ROWS, NODES], BF16)
+        param = shared.tile([P, ROWS, NODES], BF16, tag="param", align_bytes=64)
         param_rows = adj_param.rearrange("(b p) v -> p b v", p=P)
         for b in range(ROWS):
             nc.sync.dma_start(out=param[:, b, :], in_=param_rows[:, b, :])
@@ -64,24 +69,25 @@ def tile_dynamicgraphspatialconv_pb_kernel(tc, x, adj_param, tx1, cheb01, w_cheb
         def load_tx1(t):
             nc.sync.dma_start(out=tx1_raw[:, t], in_=tx1[0, t].rearrange("(b p) c -> p b c", p=P))
 
-        x_sb = keep.tile([P, PACK, NODES, STEPS], BF16)
-        x_rows = x[0].rearrange("(m p) v t -> p m v t", p=P)
+        x_sb = keep.tile([P, PACK, NODES * STEPS], BF16)
+        x_rows = x[0].rearrange("(m p) v t -> p m (v t)", p=P)
 
         def load_x(first, end):
-            nc.sync.dma_start(out=x_sb[:, :, first:end, :], in_=x_rows[:, :, first:end, :])
+            cols = slice(first * STEPS, end * STEPS)
+            nc.sync.dma_start(out=x_sb[:, :, cols], in_=x_rows[:, :, cols])
 
         load_tx1(0)
         w_raw = const.tile([P, PACK, C_OUT], BF16)
         nc.sync.dma_start(out=w_raw[:], in_=w_cheb2.rearrange("(m p) o -> p m o", p=P))
         nc.sync.dma_start(out=bias_rows[0:1, :], in_=cheb_bias.rearrange("(r o) -> r o", r=1))
-        load_tx1(1)
         load_x(0, 256)
+        load_tx1(1)
         load_tx1(2)
         load_x(256, 512)
         load_x(512, NODES)
         cheb_raw = keep.tile([P, STEPS, ROWS, C_OUT], BF16)
         for t in range(STEPS):
-            nc.sync.dma_start(out=cheb_raw[:, t], in_=cheb01[0, t].rearrange("(p b) o -> p b o", p=P))
+            nc.sync.dma_start(out=cheb_raw[:, t], in_=cheb01[0, t].rearrange("(b p) o -> p b o", p=P))
 
         ident_f = const.tile([P, P], F32)
         make_identity(nc, ident_f[:])
@@ -92,8 +98,9 @@ def tile_dynamicgraphspatialconv_pb_kernel(tc, x, adj_param, tx1, cheb01, w_cheb
             out=off_diag[:], in0=ident_f[:], scalar1=-1.0, scalar2=1.0, op0=ALU.mult, op1=ALU.add
         )
 
-        sig = keep.tile([P, ROWS, NODES], F32)
+        sig = shared.tile([P, ROWS, NODES], F32, tag="shared")
         both = keep.tile([P, ROWS, NODES], F32)
+        early_words = keep.tile([P, EARLY, P * STEPS, PACK], BF16)
         row_sums = const.tile([P, ROWS, QUARTERS], F32)
         nc.vector.memset(row_sums[:], 0.0)
 
@@ -150,6 +157,23 @@ def tile_dynamicgraphspatialconv_pb_kernel(tc, x, adj_param, tx1, cheb01, w_cheb
                 in_=tx1_grouped[(t, g)][:].rearrange("p c j -> p (c j)"),
             )
 
+        x_words = [early_words[:, r] for r in range(EARLY)]
+
+        def lay_views(r, first, end):
+            cols = slice(r * P * STEPS + first, r * P * STEPS + end)
+            return grouped_view(x_words[r][:, first:end, :]), rows_view(x_sb[:, :, cols])
+
+        def lay_x(r, who, pieces=1):
+            step = P * STEPS // pieces
+            for first in range(0, P * STEPS, step):
+                dst, src = lay_views(r, first, first + step)
+                if who == "scalar":
+                    nc.scalar.copy(out=dst, in_=src)
+                elif who == "vector":
+                    nc.vector.tensor_copy(out=dst, in_=src)
+                else:
+                    nc.gpsimd.tensor_scalar(out=dst, in0=src, scalar1=1.0, scalar2=0.0, op0=ALU.mult, op1=ALU.add)
+
         top = range(0, PACK)
         bottom = range(PACK, ROWS)
         for first in (0, 2):
@@ -164,23 +188,22 @@ def tile_dynamicgraphspatialconv_pb_kernel(tc, x, adj_param, tx1, cheb01, w_cheb
             sigmoid_piece(b, 4, 4)
         for b in bottom:
             symmetrise(b, 4, 4)
-        regroup_on_gpsimd(0, 0)
-        regroup_on_gpsimd(1, 0)
-        regroup_on_gpsimd(1, 1)
-        regroup_on_gpsimd(2, 1)
         for b in top:
             sigmoid_piece(b, 4, 4)
         for b in bottom:
             sigmoid_piece(b, 0, 4)
+        table_warm = const.tile([P, 1], F32)
+        nc.scalar.activation(out=table_warm[:], in_=sig[:, ROWS - 1, 0:1], func=ACT.Sqrt)
+        for tg in GREG:
+            regroup_on_gpsimd(*tg)
         for first in (4, 6):
             for b in (first, first + 1):
                 symmetrise(b, 0, 4)
             for b in top:
                 symmetrise(b, first, 2)
-        table_warm = const.tile([P, 1], F32)
-        nc.scalar.activation(out=table_warm[:], in_=sig[:, ROWS - 1, 0:1], func=ACT.Sqrt)
-        regroup_on_scalar(0, 1, 0)
-        regroup_on_scalar(0, 1, 1)
+
+        for a in HEADLAY:
+            lay_x(*a)
 
         bias_turned = banks.tile([P, P], BF16, tag="bank")
         nc.tensor.transpose(out=bias_turned[:], in_=bias_rows[:], identity=ident_b[:])
@@ -217,21 +240,25 @@ def tile_dynamicgraphspatialconv_pb_kernel(tc, x, adj_param, tx1, cheb01, w_cheb
 
         s_codes = keep.tile([P, TILES, PASSES, P], U32, align_bytes=64)
         s_scales = keep.tile([P, TILES, PASSES, P], U8, align_bytes=64)
-        tx2_codes = keep.tile([P, STEPS, NODES], U32, align_bytes=64)
+        tx2_codes = shared.tile([P, STEPS, NODES], U32, tag="param", name="tx2_codes", align_bytes=64)
         tx2_scales = keep.tile([P, STEPS, NODES], U8, align_bytes=64)
-        cheb_t = keep.tile([P, STEPS, NODES], BF16)
+        cheb_t = keep.tile([P, NODES, STEPS], BF16)
+        late = shared.tile([P, TILES - EARLY, P * STEPS, PACK], BF16, tag="shared", name="late")
+        x_words.extend(late[:, i] for i in range(TILES - EARLY))
         scaled = {}
         s_grouped = {}
         acc = {}
         tx2_grouped = {}
 
-        def turn_cheb(t):
-            turned = banks.tile([P, ROWS, P], BF16, tag="bank", name="cheb_turned")
-            for b in range(ROWS):
-                nc.tensor.transpose(out=turned[:, b, :], in_=cheb_raw[:, t, b, :], identity=ident_b[:])
-            nc.scalar.copy(
-                out=cheb_t[:, t, :].rearrange("p (w b) -> p w b", b=ROWS), in_=turned[:].rearrange("p b w -> p w b")
-            )
+        def turn_cheb(r):
+            turned = banks.tile([P, 2, STEPS, P], BF16, tag="bank", name="cheb_turned")
+            for i in range(2):
+                for t in range(STEPS):
+                    nc.tensor.transpose(out=turned[:, i, t, :], in_=cheb_raw[:, t, r + i, :], identity=ident_b[:])
+            for i in range(2):
+                nc.scalar.copy(
+                    out=cheb_t[:, (r + i) * P : (r + i + 1) * P, :], in_=turned[:, i].rearrange("p t v -> p v t")
+                )
 
         def scale_rows(r):
             scaled[r] = stage.tile([P, ROWS, P], F32, name="scaled")
@@ -274,21 +301,13 @@ def tile_dynamicgraphspatialconv_pb_kernel(tc, x, adj_param, tx1, cheb01, w_cheb
                         stop=(g == PASSES - 1),
                     )
 
-        x_words = {}
-
-        def lay_x(t, r):
-            x_words[(t, r)] = ahead.tile([P, P, PACK], BF16, name="x_words")
-            nc.scalar.copy(
-                out=grouped_view(x_words[(t, r)][:]), in_=rows_view(x_sb[:, :, r * P : (r + 1) * P, t])
-            )
-
         def subtract_x(t, r):
             tx2_grouped[(t, r)] = stage.tile([P, P, PACK], BF16, align_bytes=64, name="tx2_grouped")
             nc.vector.scalar_tensor_tensor(
                 out=tx2_grouped[(t, r)][:],
                 in0=acc[(t, r)][:].rearrange("p m v -> p v m"),
                 scalar=2.0,
-                in1=x_words[(t, r)][:],
+                in1=x_words[r].rearrange("p (v t) m -> p v t m", t=STEPS)[:, :, t, :],
                 op0=ALU.mult,
                 op1=ALU.subtract,
             )
@@ -319,7 +338,7 @@ def tile_dynamicgraphspatialconv_pb_kernel(tc, x, adj_param, tx1, cheb01, w_cheb
                     out=answer[:],
                     in0=mixed[:].rearrange("p u v -> p v u"),
                     scalar=bias_col[:, 0:1],
-                    in1=cheb_t[:, :, nodes].rearrange("p u v -> p v u"),
+                    in1=cheb_t[:, nodes, :],
                     op0=ALU.add,
                     op1=ALU.add,
                 )
@@ -329,34 +348,45 @@ def tile_dynamicgraphspatialconv_pb_kernel(tc, x, adj_param, tx1, cheb01, w_cheb
             nc.scalar.activation(
                 out=biased[:], in_=mixed[:].rearrange("p u v -> p v u"), func=ACT.Identity, bias=bias_col[:, 0:1]
             )
-            nc.gpsimd.tensor_tensor(
-                out=answer[:], in0=biased[:], in1=cheb_t[:, :, nodes].rearrange("p u v -> p v u"), op=ALU.add
-            )
+            for h in range(2):
+                part = slice(h * P // 2, (h + 1) * P // 2)
+                nc.gpsimd.tensor_tensor(
+                    out=answer[:, part, :],
+                    in0=biased[:, part, :],
+                    in1=cheb_t[:, r * P + h * P // 2 : r * P + (h + 1) * P // 2, :],
+                    op=ALU.add,
+                )
             nc.sync.dma_start(out=out[0, :, nodes, :], in_=answer[:])
 
         waiting = []
+        ready = []
 
         def quantise_one():
             if waiting:
                 t, r = waiting.pop(0)
                 quantise_tx2(t, r)
                 if t == last:
-                    finish(r)
+                    ready.append(r)
 
         def slot_items(k):
             return [(t, k - LAGS[t]) for t in ORDER if 0 <= k - LAGS[t] < TILES]
 
+        def scalar_slot(k):
+            for a in SPLAN.get(k, ()):
+                if a[0] == "s":
+                    scale_rows(a[1])
+                elif a[0] == "l":
+                    lay_x(a[1], "scalar")
+                else:
+                    regroup_on_scalar(*a[1:])
+            for r in GLAY.get(k, ()):
+                lay_x(r, "gpsimd", 4)
+
         last = STEPS - 1
-        scale_rows(0)
-        scale_rows(1)
+        scalar_slot(-1)
         for k in range(TILES + LAGS[last]):
             items = slot_items(k)
-            if k + 2 < TILES:
-                if k < 2:
-                    regroup_on_scalar(last, 0, k)
-                scale_rows(k + 2)
-            for item in items:
-                first_product(*item)
+            scalar_slot(k)
             extra = []
             if k < TILES:
                 scale_columns(k, 0)
@@ -377,8 +407,11 @@ def tile_dynamicgraphspatialconv_pb_kernel(tc, x, adj_param, tx1, cheb01, w_cheb
             if k + 1 in LAGS[1:]:
                 for g in range(PASSES):
                     quantise_tx1(LAGS.index(k + 1), g)
+            if k >= LAGS[last] and (k - LAGS[last]) % 2 == 0 and k - LAGS[last] < TILES:
+                turn_cheb(k - LAGS[last])
             for item in slot_items(k + 1):
-                lay_x(*item)
-            if 0 <= LAGS[last] - k < STEPS:
-                turn_cheb(LAGS[last] - k)
+                first_product(*item)
+            while ready:
+                finish(ready.pop(0))
         quantise_one()
+        finish(ready.pop(0))

@@ -142,9 +142,18 @@ def tile_dynamicgraphspatialconv_pb_kernel(tc, x, adj_param, tx1, cheb01, w_cheb
             )
 
         def regroup_on_gpsimd(t, g):
+            if (t, g) not in tx1_grouped:
+                tx1_grouped[(t, g)] = early.tile([P, C_IN, PACK], BF16, align_bytes=64, name="tx1_grouped")
             for first in range(0, C_IN, P):
-                dst, rows = regroup_views(t, g, first, first + P)
-                nc.gpsimd.tensor_scalar(out=dst, in0=rows, scalar1=1.0, scalar2=0.0, op0=ALU.mult, op1=ALU.add)
+                cols = slice(first, first + P)
+                nc.gpsimd.tensor_scalar(
+                    out=tx1_grouped[(t, g)][:, cols, :],
+                    in0=tx1_raw[:, t, g * PACK : (g + 1) * PACK, cols].rearrange("p j c -> p c j"),
+                    scalar1=1.0,
+                    scalar2=0.0,
+                    op0=ALU.mult,
+                    op1=ALU.add,
+                )
 
         def regroup_on_scalar(t, g, half):
             dst, rows = regroup_views(t, g, half * C_IN // 2, (half + 1) * C_IN // 2)
@@ -167,6 +176,10 @@ def tile_dynamicgraphspatialconv_pb_kernel(tc, x, adj_param, tx1, cheb01, w_cheb
             step = P * STEPS // pieces
             for first in range(0, P * STEPS, step):
                 dst, src = lay_views(r, first, first + step)
+                if who == "gpsimd":
+                    dst = x_words[r][:, first : first + step, :]
+                    cols = slice(r * P * STEPS + first, r * P * STEPS + first + step)
+                    src = x_sb[:, :, cols].rearrange("p m c -> p c m")
                 if who == "scalar":
                     nc.scalar.copy(out=dst, in_=src)
                 elif who == "vector":
@@ -212,16 +225,14 @@ def tile_dynamicgraphspatialconv_pb_kernel(tc, x, adj_param, tx1, cheb01, w_cheb
         nc.vector.tensor_reduce(out=deg2[:], in_=row_sums[:], axis=mybir.AxisListType.X, op=ALU.add)
         root = const.tile([P, ROWS], F32)
         nc.scalar.activation(out=root[:], in_=deg2[:], func=ACT.Sqrt, scale=-1.0)
+        w_grouped = const.tile([P, C_OUT, PACK], BF16, align_bytes=64)
+        nc.vector.tensor_copy(out=w_grouped[:], in_=w_raw[:].rearrange("p m o -> p o m"))
         rnorm = const.tile([P, ROWS], F32)
         nc.vector.reciprocal(out=rnorm[:], in_=root[:])
         quantise_tx1(0, 0)
-        w_grouped = const.tile([P, C_OUT, PACK], BF16, align_bytes=64)
         w_codes = const.tile([P, C_OUT], U32, align_bytes=64)
         w_scales = const.tile([P, C_OUT], U8, align_bytes=64)
         bias_col = const.tile([P, 1], F32)
-
-        def group_w():
-            nc.vector.tensor_copy(out=w_grouped[:], in_=w_raw[:].rearrange("p m o -> p o m"))
 
         def quantise_w():
             nc.vector.quantize_mx(
@@ -393,9 +404,7 @@ def tile_dynamicgraphspatialconv_pb_kernel(tc, x, adj_param, tx1, cheb01, w_cheb
                 extra = [lambda: scale_columns(k, 1), lambda: quantise_s(k)]
             if k == 0:
                 quantise_tx1(0, 1)
-                extra.insert(1, group_w)
-            if k == 1:
-                quantise_w()
+                extra.insert(1, quantise_w)
             for n, item in enumerate(items):
                 subtract_x(*item)
                 quantise_one()

@@ -22,12 +22,12 @@ PASSES = NODES // (P * PACK)
 HALF = 512
 HALVES = NODES // HALF
 TILES = NODES // P
-EARLY = 2
 RUN = 4
-GREG = ((0, 0), (0, 1), (1, 0), (1, 1))
-HEADLAY = ((0, "scalar"),)
-SPLAN = {-1: (("s", 0), ("s", 1)), 0: (("l", 1), ("s", 2)), 1: (("t", 2, 0, 0), ("t", 2, 0, 1), ("s", 3)), 2: (("t", 2, 1, 0), ("t", 2, 1, 1), ("s", 4)), 3: (("s", 5), ("l", 4)), 4: (("s", 6),), 5: (("s", 7), ("l", 7))}
-GLAY = {0: (2, 3), 2: (5,), 3: (6,)}
+GREG = ((0, 0),)
+SHEAD = ((0, 1, 0), (0, 1, 1))
+SPLAN = {-1: (("s", 0), ("s", 1)), 0: (("t", 1, 1, 0), ("t", 1, 1, 1), ("s", 2)), 1: (("t", 2, 0, 0), ("t", 2, 0, 1), ("s", 3)), 2: (("t", 2, 1, 0), ("t", 2, 1, 1), ("s", 4)), 3: (("s", 5),), 4: (("s", 6),), 5: (("s", 7),)}
+VREG = {1: (1, 0)}
+VFIN = 2
 QUARTERS = 4
 LAGS = (1, 2, 4)
 ORDER = (1, 0, 2)
@@ -50,7 +50,7 @@ def tile_dynamicgraphspatialconv_pb_kernel(tc, x, adj_param, tx1, cheb01, w_cheb
         const = ctx.enter_context(tc.tile_pool(name="const", bufs=1))
         keep = ctx.enter_context(tc.tile_pool(name="keep", bufs=1))
         stage = ctx.enter_context(tc.tile_pool(name="stage", bufs=3))
-        leave = ctx.enter_context(tc.tile_pool(name="leave", bufs=4))
+        leave = ctx.enter_context(tc.tile_pool(name="leave", bufs=5))
         shared = ctx.enter_context(tc.tile_pool(name="shared", bufs=1))
         early = ctx.enter_context(tc.tile_pool(name="early", bufs=5))
         banks = ctx.enter_context(tc.psum_pool(name="banks", bufs=4))
@@ -98,9 +98,8 @@ def tile_dynamicgraphspatialconv_pb_kernel(tc, x, adj_param, tx1, cheb01, w_cheb
             out=off_diag[:], in0=ident_f[:], scalar1=-1.0, scalar2=1.0, op0=ALU.mult, op1=ALU.add
         )
 
-        sig = shared.tile([P, ROWS, NODES], F32, tag="shared")
+        sig = keep.tile([P, ROWS, NODES], F32)
         both = keep.tile([P, ROWS, NODES], F32)
-        early_words = keep.tile([P, EARLY, P * STEPS, PACK], BF16)
         row_sums = const.tile([P, ROWS, QUARTERS], F32)
         nc.vector.memset(row_sums[:], 0.0)
 
@@ -142,18 +141,8 @@ def tile_dynamicgraphspatialconv_pb_kernel(tc, x, adj_param, tx1, cheb01, w_cheb
             )
 
         def regroup_on_gpsimd(t, g):
-            if (t, g) not in tx1_grouped:
-                tx1_grouped[(t, g)] = early.tile([P, C_IN, PACK], BF16, align_bytes=64, name="tx1_grouped")
-            for first in range(0, C_IN, P):
-                cols = slice(first, first + P)
-                nc.gpsimd.tensor_scalar(
-                    out=tx1_grouped[(t, g)][:, cols, :],
-                    in0=tx1_raw[:, t, g * PACK : (g + 1) * PACK, cols].rearrange("p j c -> p c j"),
-                    scalar1=1.0,
-                    scalar2=0.0,
-                    op0=ALU.mult,
-                    op1=ALU.add,
-                )
+            dst, rows = regroup_views(t, g, 0, C_IN)
+            nc.gpsimd.tensor_scalar(out=dst, in0=rows, scalar1=1.0, scalar2=0.0, op0=ALU.mult, op1=ALU.add)
 
         def regroup_on_scalar(t, g, half):
             dst, rows = regroup_views(t, g, half * C_IN // 2, (half + 1) * C_IN // 2)
@@ -165,27 +154,6 @@ def tile_dynamicgraphspatialconv_pb_kernel(tc, x, adj_param, tx1, cheb01, w_cheb
                 scales=tx1_scales[:, t, g, :],
                 in_=tx1_grouped[(t, g)][:].rearrange("p c j -> p (c j)"),
             )
-
-        x_words = [early_words[:, r] for r in range(EARLY)]
-
-        def lay_views(r, first, end):
-            cols = slice(r * P * STEPS + first, r * P * STEPS + end)
-            return grouped_view(x_words[r][:, first:end, :]), rows_view(x_sb[:, :, cols])
-
-        def lay_x(r, who, pieces=1):
-            step = P * STEPS // pieces
-            for first in range(0, P * STEPS, step):
-                dst, src = lay_views(r, first, first + step)
-                if who == "gpsimd":
-                    dst = x_words[r][:, first : first + step, :]
-                    cols = slice(r * P * STEPS + first, r * P * STEPS + first + step)
-                    src = x_sb[:, :, cols].rearrange("p m c -> p c m")
-                if who == "scalar":
-                    nc.scalar.copy(out=dst, in_=src)
-                elif who == "vector":
-                    nc.vector.tensor_copy(out=dst, in_=src)
-                else:
-                    nc.gpsimd.tensor_scalar(out=dst, in0=src, scalar1=1.0, scalar2=0.0, op0=ALU.mult, op1=ALU.add)
 
         top = range(0, PACK)
         bottom = range(PACK, ROWS)
@@ -207,6 +175,8 @@ def tile_dynamicgraphspatialconv_pb_kernel(tc, x, adj_param, tx1, cheb01, w_cheb
             sigmoid_piece(b, 0, 4)
         table_warm = const.tile([P, 1], F32)
         nc.scalar.activation(out=table_warm[:], in_=sig[:, ROWS - 1, 0:1], func=ACT.Sqrt)
+        for a in SHEAD:
+            regroup_on_scalar(*a)
         for tg in GREG:
             regroup_on_gpsimd(*tg)
         for first in (4, 6):
@@ -215,19 +185,17 @@ def tile_dynamicgraphspatialconv_pb_kernel(tc, x, adj_param, tx1, cheb01, w_cheb
             for b in top:
                 symmetrise(b, first, 2)
 
-        for a in HEADLAY:
-            lay_x(*a)
-
         bias_turned = banks.tile([P, P], BF16, tag="bank")
         nc.tensor.transpose(out=bias_turned[:], in_=bias_rows[:], identity=ident_b[:])
 
         deg2 = const.tile([P, ROWS], F32)
         nc.vector.tensor_reduce(out=deg2[:], in_=row_sums[:], axis=mybir.AxisListType.X, op=ALU.add)
-        root = const.tile([P, ROWS], F32)
-        nc.scalar.activation(out=root[:], in_=deg2[:], func=ACT.Sqrt, scale=-1.0)
+        root = const.tile([P, 2, ROWS], F32)
+        for i, scale in enumerate((-1.0, -0.25)):
+            nc.scalar.activation(out=root[:, i, :], in_=deg2[:], func=ACT.Sqrt, scale=scale)
         w_grouped = const.tile([P, C_OUT, PACK], BF16, align_bytes=64)
         nc.vector.tensor_copy(out=w_grouped[:], in_=w_raw[:].rearrange("p m o -> p o m"))
-        rnorm = const.tile([P, ROWS], F32)
+        rnorm = const.tile([P, 2, ROWS], F32)
         nc.vector.reciprocal(out=rnorm[:], in_=root[:])
         quantise_tx1(0, 0)
         w_codes = const.tile([P, C_OUT], U32, align_bytes=64)
@@ -246,7 +214,7 @@ def tile_dynamicgraphspatialconv_pb_kernel(tc, x, adj_param, tx1, cheb01, w_cheb
             for i in range(PACK):
                 r = half * PACK + i
                 nc.tensor.transpose(
-                    out=factor[half][:, i, :], in_=rnorm[:, r : r + 1].to_broadcast([P, P]), identity=ident_f[:]
+                    out=factor[half][:, i, :], in_=rnorm[:, 1, r : r + 1].to_broadcast([P, P]), identity=ident_f[:]
                 )
 
         s_codes = keep.tile([P, TILES, PASSES, P], U32, align_bytes=64)
@@ -254,8 +222,6 @@ def tile_dynamicgraphspatialconv_pb_kernel(tc, x, adj_param, tx1, cheb01, w_cheb
         tx2_codes = shared.tile([P, STEPS, NODES], U32, tag="param", name="tx2_codes", align_bytes=64)
         tx2_scales = keep.tile([P, STEPS, NODES], U8, align_bytes=64)
         cheb_t = keep.tile([P, NODES, STEPS], BF16)
-        late = shared.tile([P, TILES - EARLY, P * STEPS, PACK], BF16, tag="shared", name="late")
-        x_words.extend(late[:, i] for i in range(TILES - EARLY))
         scaled = {}
         s_grouped = {}
         acc = {}
@@ -275,7 +241,7 @@ def tile_dynamicgraphspatialconv_pb_kernel(tc, x, adj_param, tx1, cheb01, w_cheb
             scaled[r] = stage.tile([P, ROWS, P], F32, name="scaled")
             for b in range(ROWS):
                 nc.scalar.activation(
-                    out=scaled[r][:, b, :], in_=both[:, b, r * P : (r + 1) * P], func=ACT.Copy, scale=rnorm[:, b : b + 1]
+                    out=scaled[r][:, b, :], in_=both[:, b, r * P : (r + 1) * P], func=ACT.Copy, scale=rnorm[:, 0, b : b + 1]
                 )
 
         def scale_columns(r, g):
@@ -314,13 +280,12 @@ def tile_dynamicgraphspatialconv_pb_kernel(tc, x, adj_param, tx1, cheb01, w_cheb
 
         def subtract_x(t, r):
             tx2_grouped[(t, r)] = stage.tile([P, P, PACK], BF16, align_bytes=64, name="tx2_grouped")
-            nc.vector.scalar_tensor_tensor(
-                out=tx2_grouped[(t, r)][:],
-                in0=acc[(t, r)][:].rearrange("p m v -> p v m"),
-                scalar=2.0,
-                in1=x_words[r].rearrange("p (v t) m -> p v t m", t=STEPS)[:, :, t, :],
-                op0=ALU.mult,
-                op1=ALU.subtract,
+            x_tile = x_sb[:, :, r * P * STEPS : (r + 1) * P * STEPS].rearrange("p m (v t) -> p m v t", t=STEPS)
+            nc.vector.tensor_tensor(
+                out=grouped_view(tx2_grouped[(t, r)][:]),
+                in0=rows_view(acc[(t, r)][:]),
+                in1=rows_view(x_tile[:, :, :, t]),
+                op=ALU.subtract,
             )
 
         def quantise_tx2(t, r):
@@ -344,7 +309,7 @@ def tile_dynamicgraphspatialconv_pb_kernel(tc, x, adj_param, tx1, cheb01, w_cheb
                     stop=True,
                 )
             answer = leave.tile([P, P, STEPS], F32)
-            if r == TILES - 1:
+            if r >= TILES - VFIN:
                 nc.vector.scalar_tensor_tensor(
                     out=answer[:],
                     in0=mixed[:].rearrange("p u v -> p v u"),
@@ -386,12 +351,8 @@ def tile_dynamicgraphspatialconv_pb_kernel(tc, x, adj_param, tx1, cheb01, w_cheb
             for a in SPLAN.get(k, ()):
                 if a[0] == "s":
                     scale_rows(a[1])
-                elif a[0] == "l":
-                    lay_x(a[1], "scalar")
                 else:
                     regroup_on_scalar(*a[1:])
-            for r in GLAY.get(k, ()):
-                lay_x(r, "gpsimd", 4)
 
         last = STEPS - 1
         scalar_slot(-1)
@@ -402,6 +363,9 @@ def tile_dynamicgraphspatialconv_pb_kernel(tc, x, adj_param, tx1, cheb01, w_cheb
             if k < TILES:
                 scale_columns(k, 0)
                 extra = [lambda: scale_columns(k, 1), lambda: quantise_s(k)]
+            if k in VREG:
+                dst, rows = regroup_views(*VREG[k], 0, C_IN)
+                nc.vector.tensor_copy(out=dst, in_=rows)
             if k == 0:
                 quantise_tx1(0, 1)
                 extra.insert(1, quantise_w)
@@ -420,7 +384,8 @@ def tile_dynamicgraphspatialconv_pb_kernel(tc, x, adj_param, tx1, cheb01, w_cheb
                 turn_cheb(k - LAGS[last])
             for item in slot_items(k + 1):
                 first_product(*item)
-            while ready:
+            while ready and ready[0] < TILES - VFIN:
                 finish(ready.pop(0))
         quantise_one()
-        finish(ready.pop(0))
+        for r in ready:
+            finish(r)

@@ -21,26 +21,25 @@ ROWS = NODES // P
 PASSES = NODES // (P * PACK)
 HALF = 512
 HALVES = NODES // HALF
+PAIRS = NODES // (2 * P)
 TILES = NODES // P
 RUN = 4
+SMIR = (6, 7)
 GREG = ((0, 0),)
-SHEAD = ((0, 1, 0), (0, 1, 1))
-SPLAN = {-1: (("s", 0), ("s", 1)), 0: (("t", 1, 1, 0), ("t", 1, 1, 1), ("s", 2)), 1: (("t", 2, 0, 0), ("t", 2, 0, 1), ("s", 3)), 2: (("t", 2, 1, 0), ("t", 2, 1, 1), ("s", 4)), 3: (("s", 5),), 4: (("s", 6),), 5: (("s", 7),)}
-VREG = {1: (1, 0)}
+GP = 1
+PAIR = 2
 VFIN = 2
 QUARTERS = 4
-LAGS = (1, 2, 4)
-ORDER = (1, 0, 2)
 
 FLOPS = 2 * STEPS * NODES * NODES * C_IN + 2 * STEPS * NODES * C_IN * C_OUT
 
 
-def grouped_view(dst):
-    return dst.rearrange("p (c i) j -> p c j i", i=RUN)
+def grouped_view(dst, run=RUN):
+    return dst.rearrange("p (c i) j -> p c j i", i=run)
 
 
-def rows_view(src):
-    return src.rearrange("p j (c i) -> p c j i", i=RUN)
+def rows_view(src, run=RUN):
+    return src.rearrange("p j (c i) -> p c j i", i=run)
 
 
 def tile_dynamicgraphspatialconv_pb_kernel(tc, x, adj_param, tx1, cheb01, w_cheb2, cheb_bias, out):
@@ -50,9 +49,9 @@ def tile_dynamicgraphspatialconv_pb_kernel(tc, x, adj_param, tx1, cheb01, w_cheb
         const = ctx.enter_context(tc.tile_pool(name="const", bufs=1))
         keep = ctx.enter_context(tc.tile_pool(name="keep", bufs=1))
         stage = ctx.enter_context(tc.tile_pool(name="stage", bufs=3))
-        leave = ctx.enter_context(tc.tile_pool(name="leave", bufs=5))
+        leave = ctx.enter_context(tc.tile_pool(name="leave", bufs=8))
         shared = ctx.enter_context(tc.tile_pool(name="shared", bufs=1))
-        early = ctx.enter_context(tc.tile_pool(name="early", bufs=5))
+        early = ctx.enter_context(tc.tile_pool(name="early", bufs=4))
         banks = ctx.enter_context(tc.psum_pool(name="banks", bufs=4))
         results = ctx.enter_context(tc.psum_pool(name="results", bufs=2))
         factors = ctx.enter_context(tc.psum_pool(name="factors", bufs=2))
@@ -98,7 +97,7 @@ def tile_dynamicgraphspatialconv_pb_kernel(tc, x, adj_param, tx1, cheb01, w_cheb
             out=off_diag[:], in0=ident_f[:], scalar1=-1.0, scalar2=1.0, op0=ALU.mult, op1=ALU.add
         )
 
-        sig = keep.tile([P, ROWS, NODES], F32)
+        sig = shared.tile([P, ROWS, NODES], F32, tag="sig", align_bytes=64)
         both = keep.tile([P, ROWS, NODES], F32)
         row_sums = const.tile([P, ROWS, QUARTERS], F32)
         nc.vector.memset(row_sums[:], 0.0)
@@ -141,8 +140,9 @@ def tile_dynamicgraphspatialconv_pb_kernel(tc, x, adj_param, tx1, cheb01, w_cheb
             )
 
         def regroup_on_gpsimd(t, g):
-            dst, rows = regroup_views(t, g, 0, C_IN)
-            nc.gpsimd.tensor_scalar(out=dst, in0=rows, scalar1=1.0, scalar2=0.0, op0=ALU.mult, op1=ALU.add)
+            for i in range(GP):
+                dst, rows = regroup_views(t, g, i * C_IN // GP, (i + 1) * C_IN // GP)
+                nc.gpsimd.tensor_scalar(out=dst, in0=rows, scalar1=1.0, scalar2=0.0, op0=ALU.mult, op1=ALU.add)
 
         def regroup_on_scalar(t, g, half):
             dst, rows = regroup_views(t, g, half * C_IN // 2, (half + 1) * C_IN // 2)
@@ -169,21 +169,39 @@ def tile_dynamicgraphspatialconv_pb_kernel(tc, x, adj_param, tx1, cheb01, w_cheb
             sigmoid_piece(b, 4, 4)
         for b in bottom:
             symmetrise(b, 4, 4)
-        for b in top:
-            sigmoid_piece(b, 4, 4)
         for b in bottom:
             sigmoid_piece(b, 0, 4)
+        for b in top:
+            sigmoid_piece(b, 4, 4)
         table_warm = const.tile([P, 1], F32)
-        nc.scalar.activation(out=table_warm[:], in_=sig[:, ROWS - 1, 0:1], func=ACT.Sqrt)
-        for a in SHEAD:
-            regroup_on_scalar(*a)
+        nc.scalar.activation(out=table_warm[:], in_=sig[:, PACK - 1, NODES - 1 : NODES], func=ACT.Sqrt)
+        w_grouped = const.tile([P, C_OUT, PACK], BF16, align_bytes=64)
+        nc.scalar.copy(out=grouped_view(w_grouped[:]), in_=rows_view(w_raw[:]))
         for tg in GREG:
             regroup_on_gpsimd(*tg)
-        for first in (4, 6):
-            for b in (first, first + 1):
-                symmetrise(b, 0, 4)
-            for b in top:
-                symmetrise(b, first, 2)
+        mirrored = {b: (results if b < 6 else factors).tile([P, PACK, P], F32, tag="mirrored", name="mirrored") for b in bottom}
+        for i in top:
+            symmetrise(i, 4, 4)
+        for i in top:
+            for b in bottom:
+                nc.tensor.transpose(
+                    out=mirrored[b][:, i, :], in_=both[:, i, b * P : (b + 1) * P], identity=ident_f[:]
+                )
+        tx1_grouped[(0, 1)] = early.tile([P, C_IN, PACK], BF16, align_bytes=64, name="tx1_grouped")
+        nc.vector.tensor_copy(
+            out=tx1_grouped[(0, 1)][:], in_=tx1_raw[:, 0, PACK:, :].rearrange("p j c -> p c j")
+        )
+        for b in bottom:
+            if b in SMIR:
+                spare = stage.tile([P, PACK, P], BF16, name="spare", bufs=1)
+                nc.scalar.activation(out=spare[:], in_=mirrored[b][:], func=ACT.Copy, accum_out=row_sums[:, b, 0:1])
+            else:
+                nc.vector.tensor_reduce(
+                    out=row_sums[:, b, 0:1],
+                    in_=mirrored[b][:].rearrange("p i w -> p (i w)"),
+                    axis=mybir.AxisListType.X,
+                    op=ALU.add,
+                )
 
         bias_turned = banks.tile([P, P], BF16, tag="bank")
         nc.tensor.transpose(out=bias_turned[:], in_=bias_rows[:], identity=ident_b[:])
@@ -193,37 +211,34 @@ def tile_dynamicgraphspatialconv_pb_kernel(tc, x, adj_param, tx1, cheb01, w_cheb
         root = const.tile([P, 2, ROWS], F32)
         for i, scale in enumerate((-1.0, -0.25)):
             nc.scalar.activation(out=root[:, i, :], in_=deg2[:], func=ACT.Sqrt, scale=scale)
-        w_grouped = const.tile([P, C_OUT, PACK], BF16, align_bytes=64)
-        nc.vector.tensor_copy(out=w_grouped[:], in_=w_raw[:].rearrange("p m o -> p o m"))
         rnorm = const.tile([P, 2, ROWS], F32)
         nc.vector.reciprocal(out=rnorm[:], in_=root[:])
-        quantise_tx1(0, 0)
+
         w_codes = const.tile([P, C_OUT], U32, align_bytes=64)
         w_scales = const.tile([P, C_OUT], U8, align_bytes=64)
         bias_col = const.tile([P, 1], F32)
+        nc.vector.tensor_copy(out=bias_col[:], in_=bias_turned[:, 0:1])
 
         def quantise_w():
             nc.vector.quantize_mx(
                 out=w_codes[:].bitcast(FP8X4), scales=w_scales[:], in_=w_grouped[:].rearrange("p o m -> p (o m)")
             )
-            nc.vector.tensor_copy(out=bias_col[:], in_=bias_turned[:, 0:1])
 
-        factor = []
-        for half in range(HALVES):
-            factor.append(factors.tile([P, PACK, P], F32, name="factor"))
+        factor = [factors.tile([P, PACK, P], F32, tag="mirrored", name="factor") for i in range(HALVES)]
+        for half in (1, 0):
             for i in range(PACK):
                 r = half * PACK + i
                 nc.tensor.transpose(
                     out=factor[half][:, i, :], in_=rnorm[:, 1, r : r + 1].to_broadcast([P, P]), identity=ident_f[:]
                 )
 
-        s_codes = keep.tile([P, TILES, PASSES, P], U32, align_bytes=64)
-        s_scales = keep.tile([P, TILES, PASSES, P], U8, align_bytes=64)
+        s_codes = keep.tile([P, PAIRS, PASSES, 2 * P], U32, align_bytes=64)
+        s_scales = keep.tile([P, PAIRS, PASSES, 2 * P], U8, align_bytes=64)
         tx2_codes = shared.tile([P, STEPS, NODES], U32, tag="param", name="tx2_codes", align_bytes=64)
         tx2_scales = keep.tile([P, STEPS, NODES], U8, align_bytes=64)
+        s_grouped = shared.tile([P, PAIRS, PASSES, 2 * P, PACK], BF16, tag="sig", name="s_grouped", align_bytes=64)
         cheb_t = keep.tile([P, NODES, STEPS], BF16)
         scaled = {}
-        s_grouped = {}
         acc = {}
         tx2_grouped = {}
 
@@ -237,31 +252,48 @@ def tile_dynamicgraphspatialconv_pb_kernel(tc, x, adj_param, tx1, cheb01, w_cheb
                     out=cheb_t[:, (r + i) * P : (r + i + 1) * P, :], in_=turned[:, i].rearrange("p t v -> p v t")
                 )
 
-        def scale_rows(r):
-            scaled[r] = stage.tile([P, ROWS, P], F32, name="scaled")
-            for b in range(ROWS):
+        def scale_rows(q, g):
+            scaled[(q, g)] = stage.tile([P, PACK, 2 * P], F32, name="scaled", bufs=4)
+            for j in range(PACK):
+                b = g * PACK + j
                 nc.scalar.activation(
-                    out=scaled[r][:, b, :], in_=both[:, b, r * P : (r + 1) * P], func=ACT.Copy, scale=rnorm[:, 0, b : b + 1]
+                    out=scaled[(q, g)][:, j, :],
+                    in_=both[:, b, 2 * q * P : 2 * (q + 1) * P],
+                    func=ACT.Copy,
+                    scale=rnorm[:, 0, b : b + 1],
                 )
 
-        def scale_columns(r, g):
-            if g == 0:
-                s_grouped[r] = stage.tile([P, PASSES, P, PACK], BF16, align_bytes=64, name="s_grouped")
+        def scale_columns(q, g):
+            columns = factor[q // 2][:].rearrange("p i v -> p (i v)")[:, (q % 2) * 2 * P : (q % 2 + 1) * 2 * P]
             nc.vector.tensor_tensor(
-                out=grouped_view(s_grouped[r][:, g]),
-                in0=rows_view(scaled[r][:, g * PACK : (g + 1) * PACK, :]),
-                in1=factor[r // PACK][:, r % PACK, :]
-                .rearrange("p (c i) -> p c i", i=RUN)
+                out=grouped_view(s_grouped[:, q, g], PAIR),
+                in0=rows_view(scaled[(q, g)][:], PAIR),
+                in1=columns.rearrange("p (c i) -> p c i", i=PAIR)
                 .unsqueeze(2)
-                .to_broadcast([P, P // RUN, PACK, RUN]),
+                .to_broadcast([P, 2 * P // PAIR, PACK, PAIR]),
                 op=ALU.mult,
             )
 
-        def quantise_s(r):
+        def mirror_s(q):
+            turned = banks.tile([P, 2, PACK, P], BF16, tag="bank", name="s_turned")
+            for i in range(2):
+                for j in range(PACK):
+                    r = PACK + j
+                    nc.tensor.transpose(
+                        out=turned[:, i, j, :],
+                        in_=s_grouped[:, r // 2, 0, (r % 2) * P : (r % 2 + 1) * P, 2 * q + i],
+                        identity=ident_b[:],
+                    )
+            for i in range(2):
+                nc.scalar.copy(
+                    out=s_grouped[:, q, 1, i * P : (i + 1) * P, :], in_=turned[:, i].rearrange("p j v -> p v j")
+                )
+
+        def quantise_s(q):
             nc.vector.quantize_mx(
-                out=s_codes[:, r].rearrange("p g v -> p (g v)").bitcast(FP8X4),
-                scales=s_scales[:, r].rearrange("p g v -> p (g v)"),
-                in_=s_grouped[r][:].rearrange("p g v j -> p (g v j)"),
+                out=s_codes[:, q].rearrange("p g v -> p (g v)").bitcast(FP8X4),
+                scales=s_scales[:, q].rearrange("p g v -> p (g v)"),
+                in_=s_grouped[:, q].rearrange("p g v j -> p (g v j)"),
             )
 
         def first_product(t, r):
@@ -272,32 +304,36 @@ def tile_dynamicgraphspatialconv_pb_kernel(tc, x, adj_param, tx1, cheb01, w_cheb
                         out=acc[(t, r)][:, m, :],
                         lhsT=tx1_codes[:, t, g, m * P : (m + 1) * P].bitcast(FP8X4),
                         lhsT_scale=tx1_scales[:, t, g, m * P : (m + 1) * P],
-                        rhs=s_codes[:, r, g, :].bitcast(FP8X4),
-                        rhs_scale=s_scales[:, r, g, :],
+                        rhs=s_codes[:, r // 2, g, (r % 2) * P : (r % 2 + 1) * P].bitcast(FP8X4),
+                        rhs_scale=s_scales[:, r // 2, g, (r % 2) * P : (r % 2 + 1) * P],
                         start=(g == 0),
                         stop=(g == PASSES - 1),
                     )
 
         def subtract_x(t, r):
-            tx2_grouped[(t, r)] = stage.tile([P, P, PACK], BF16, align_bytes=64, name="tx2_grouped")
+            if r % 2 == 0:
+                tx2_grouped[(t, r // 2)] = stage.tile([P, 2 * P, PACK], BF16, align_bytes=64, name="tx2_grouped")
+            grouped = tx2_grouped[(t, r // 2)][:, (r % 2) * P : (r % 2 + 1) * P, :]
             x_tile = x_sb[:, :, r * P * STEPS : (r + 1) * P * STEPS].rearrange("p m (v t) -> p m v t", t=STEPS)
             nc.vector.tensor_tensor(
-                out=grouped_view(tx2_grouped[(t, r)][:]),
+                out=grouped_view(grouped),
                 in0=rows_view(acc[(t, r)][:]),
                 in1=rows_view(x_tile[:, :, :, t]),
                 op=ALU.subtract,
             )
 
-        def quantise_tx2(t, r):
+        def quantise_tx2(t, first, count):
+            nodes = slice(first * P, (first + count) * P)
+            part = slice((first % 2) * P, (first % 2 + count) * P)
             nc.vector.quantize_mx(
-                out=tx2_codes[:, t, r * P : (r + 1) * P].bitcast(FP8X4),
-                scales=tx2_scales[:, t, r * P : (r + 1) * P],
-                in_=tx2_grouped[(t, r)][:].rearrange("p v m -> p (v m)"),
+                out=tx2_codes[:, t, nodes].bitcast(FP8X4),
+                scales=tx2_scales[:, t, nodes],
+                in_=tx2_grouped[(t, first // 2)][:, part, :].rearrange("p v m -> p (v m)"),
             )
 
         def finish(r):
             nodes = slice(r * P, (r + 1) * P)
-            mixed = results.tile([P, STEPS, P], F32)
+            mixed = results.tile([P, STEPS, P], F32, tag="mirrored", name="mixed")
             for u in range(STEPS):
                 nc.tensor.matmul_mx(
                     out=mixed[:, u, :],
@@ -320,7 +356,7 @@ def tile_dynamicgraphspatialconv_pb_kernel(tc, x, adj_param, tx1, cheb01, w_cheb
                 )
                 nc.sync.dma_start(out=out[0, :, nodes, :], in_=answer[:])
                 return
-            biased = leave.tile([P, P, STEPS], F32)
+            biased = leave.tile([P, P, STEPS], F32, bufs=2)
             nc.scalar.activation(
                 out=biased[:], in_=mixed[:].rearrange("p u v -> p v u"), func=ACT.Identity, bias=bias_col[:, 0:1]
             )
@@ -334,58 +370,63 @@ def tile_dynamicgraphspatialconv_pb_kernel(tc, x, adj_param, tx1, cheb01, w_cheb
                 )
             nc.sync.dma_start(out=out[0, :, nodes, :], in_=answer[:])
 
-        waiting = []
-        ready = []
-
-        def quantise_one():
-            if waiting:
-                t, r = waiting.pop(0)
-                quantise_tx2(t, r)
-                if t == last:
-                    ready.append(r)
-
-        def slot_items(k):
-            return [(t, k - LAGS[t]) for t in ORDER if 0 <= k - LAGS[t] < TILES]
-
-        def scalar_slot(k):
-            for a in SPLAN.get(k, ()):
-                if a[0] == "s":
-                    scale_rows(a[1])
-                else:
-                    regroup_on_scalar(*a[1:])
+        def regroup_twice(t, g):
+            regroup_on_scalar(t, g, 0)
+            regroup_on_scalar(t, g, 1)
 
         last = STEPS - 1
-        scalar_slot(-1)
-        for k in range(TILES + LAGS[last]):
-            items = slot_items(k)
-            scalar_slot(k)
-            extra = []
-            if k < TILES:
-                scale_columns(k, 0)
-                extra = [lambda: scale_columns(k, 1), lambda: quantise_s(k)]
-            if k in VREG:
-                dst, rows = regroup_views(*VREG[k], 0, C_IN)
-                nc.vector.tensor_copy(out=dst, in_=rows)
-            if k == 0:
-                quantise_tx1(0, 1)
-                extra.insert(1, quantise_w)
-            for n, item in enumerate(items):
-                subtract_x(*item)
-                quantise_one()
-                waiting.append(item)
-                if extra:
-                    extra.pop(0)()
-            for step in extra:
-                step()
-            if k + 1 in LAGS[1:]:
-                for g in range(PASSES):
-                    quantise_tx1(LAGS.index(k + 1), g)
-            if k >= LAGS[last] and (k - LAGS[last]) % 2 == 0 and k - LAGS[last] < TILES:
-                turn_cheb(k - LAGS[last])
-            for item in slot_items(k + 1):
-                first_product(*item)
-            while ready and ready[0] < TILES - VFIN:
-                finish(ready.pop(0))
-        quantise_one()
-        for r in ready:
+        units = [(0, 0), (0, 1), (1, 0), (0, 2), (1, 1), (2, 0), (2, 1), (0, 3), (1, 2), (2, 2), (1, 3), (2, 3)]
+
+        quantise_tx1(0, 0)
+        quantise_tx1(0, 1)
+        scale_rows(2, 0)
+        scale_rows(3, 0)
+        scale_rows(0, 0)
+        scale_rows(1, 0)
+        scale_columns(2, 0)
+        scale_columns(3, 0)
+        mirror_s(0)
+        mirror_s(1)
+        scale_columns(0, 0)
+        scale_columns(1, 0)
+        quantise_s(0)
+        first_product(0, 0)
+        first_product(0, 1)
+        regroup_twice(1, 0)
+        scale_rows(2, 1)
+        regroup_twice(1, 1)
+        scale_rows(3, 1)
+        regroup_twice(2, 0)
+        regroup_twice(2, 1)
+        quantise_w()
+        quantise_s(1)
+        first_product(0, 2)
+        first_product(0, 3)
+        plan = {
+            (0, 0): lambda: (scale_columns(2, 1), quantise_tx1(1, 0)),
+            (0, 1): lambda: (quantise_tx1(1, 1), quantise_s(2), scale_columns(3, 1)),
+            (1, 0): lambda: (quantise_s(3), turn_cheb(0)),
+            (0, 2): lambda: (quantise_tx1(2, 0), quantise_tx1(2, 1)),
+            (1, 1): lambda: turn_cheb(2),
+            (2, 1): lambda: turn_cheb(4),
+            (2, 2): lambda: turn_cheb(6),
+        }
+        waiting = None
+        for n, (t, q) in enumerate(units):
+            subtract_x(t, 2 * q)
+            if waiting:
+                quantise_tx2(waiting[0], 2 * waiting[1], 2)
+            subtract_x(t, 2 * q + 1)
+            plan.get((t, q), lambda: 0)()
+            if 1 <= n < len(units) - 1:
+                ahead = units[n + 1]
+                first_product(ahead[0], 2 * ahead[1])
+                first_product(ahead[0], 2 * ahead[1] + 1)
+            if waiting and waiting[0] == last:
+                finish(2 * waiting[1])
+                finish(2 * waiting[1] + 1)
+            waiting = (t, q)
+        for r in (TILES - 2, TILES - 1):
+            quantise_tx2(last, r, 1)
+        for r in (TILES - 2, TILES - 1):
             finish(r)

@@ -24,8 +24,8 @@ HALVES = NODES // HALF
 PAIRS = NODES // (2 * P)
 TILES = NODES // P
 RUN = 4
-SMIR = (6, 7)
-GREG = ((0, 0),)
+SMIR = (7,)
+GREG = ((0, 0), (0, 1))
 GP = 1
 PAIR = 2
 VFIN = 2
@@ -51,7 +51,7 @@ def tile_dynamicgraphspatialconv_pb_kernel(tc, x, adj_param, tx1, cheb01, w_cheb
         stage = ctx.enter_context(tc.tile_pool(name="stage", bufs=3))
         leave = ctx.enter_context(tc.tile_pool(name="leave", bufs=8))
         shared = ctx.enter_context(tc.tile_pool(name="shared", bufs=1))
-        early = ctx.enter_context(tc.tile_pool(name="early", bufs=4))
+        early = ctx.enter_context(tc.tile_pool(name="early", bufs=2))
         banks = ctx.enter_context(tc.psum_pool(name="banks", bufs=4))
         results = ctx.enter_context(tc.psum_pool(name="results", bufs=2))
         factors = ctx.enter_context(tc.psum_pool(name="factors", bufs=2))
@@ -61,8 +61,18 @@ def tile_dynamicgraphspatialconv_pb_kernel(tc, x, adj_param, tx1, cheb01, w_cheb
 
         param = shared.tile([P, ROWS, NODES], BF16, tag="param", align_bytes=64)
         param_rows = adj_param.rearrange("(b p) v -> p b v", p=P)
-        for b in range(ROWS):
-            nc.sync.dma_start(out=param[:, b, :], in_=param_rows[:, b, :])
+
+        def load_param(chunks, first, end):
+            cols = slice(first * P, end * P)
+            nc.sync.dma_start(out=param[:, chunks, cols], in_=param_rows[:, chunks, cols])
+
+        load_param(slice(0, 2), 0, 2)
+        load_param(slice(0, 2), 2, 4)
+        load_param(slice(2, 4), 0, 4)
+        load_param(slice(4, 6), 4, 8)
+        load_param(slice(6, 8), 4, 8)
+        load_param(slice(4, 8), 0, 4)
+        load_param(slice(0, 4), 4, 8)
         tx1_raw = keep.tile([P, STEPS, ROWS, C_IN], BF16)
 
         def load_tx1(t):
@@ -132,10 +142,10 @@ def tile_dynamicgraphspatialconv_pb_kernel(tc, x, adj_param, tx1, cheb01, w_cheb
         tx1_grouped = {}
 
         def regroup_views(t, g, first, end):
-            if (t, g) not in tx1_grouped:
-                tx1_grouped[(t, g)] = early.tile([P, C_IN, PACK], BF16, align_bytes=64, name="tx1_grouped")
+            if t not in tx1_grouped:
+                tx1_grouped[t] = early.tile([P, PASSES, C_IN, PACK], BF16, align_bytes=64, name="tx1_grouped")
             return (
-                grouped_view(tx1_grouped[(t, g)][:, first:end, :]),
+                grouped_view(tx1_grouped[t][:, g, first:end, :]),
                 rows_view(tx1_raw[:, t, g * PACK : (g + 1) * PACK, first:end]),
             )
 
@@ -148,11 +158,11 @@ def tile_dynamicgraphspatialconv_pb_kernel(tc, x, adj_param, tx1, cheb01, w_cheb
             dst, rows = regroup_views(t, g, half * C_IN // 2, (half + 1) * C_IN // 2)
             nc.scalar.copy(out=dst, in_=rows)
 
-        def quantise_tx1(t, g):
+        def quantise_tx1(t):
             nc.vector.quantize_mx(
-                out=tx1_codes[:, t, g, :].bitcast(FP8X4),
-                scales=tx1_scales[:, t, g, :],
-                in_=tx1_grouped[(t, g)][:].rearrange("p c j -> p (c j)"),
+                out=tx1_codes[:, t].rearrange("p g c -> p (g c)").bitcast(FP8X4),
+                scales=tx1_scales[:, t].rearrange("p g c -> p (g c)"),
+                in_=tx1_grouped[t][:].rearrange("p g c j -> p (g c j)"),
             )
 
         top = range(0, PACK)
@@ -162,9 +172,12 @@ def tile_dynamicgraphspatialconv_pb_kernel(tc, x, adj_param, tx1, cheb01, w_cheb
                 sigmoid_piece(b, first, 2)
         for b in (2, 3):
             sigmoid_piece(b, 0, 4)
-        for first in (0, 2):
-            for b in top:
-                symmetrise(b, first, 2)
+        for b in (0, 1):
+            symmetrise(b, 0, 2)
+        for b in (2, 3):
+            symmetrise(b, 0, 4)
+        for b in (0, 1):
+            symmetrise(b, 2, 2)
         for b in bottom:
             sigmoid_piece(b, 4, 4)
         for b in bottom:
@@ -187,11 +200,7 @@ def tile_dynamicgraphspatialconv_pb_kernel(tc, x, adj_param, tx1, cheb01, w_cheb
                 nc.tensor.transpose(
                     out=mirrored[b][:, i, :], in_=both[:, i, b * P : (b + 1) * P], identity=ident_f[:]
                 )
-        tx1_grouped[(0, 1)] = early.tile([P, C_IN, PACK], BF16, align_bytes=64, name="tx1_grouped")
-        nc.vector.tensor_copy(
-            out=tx1_grouped[(0, 1)][:], in_=tx1_raw[:, 0, PACK:, :].rearrange("p j c -> p c j")
-        )
-        for b in bottom:
+        def sum_mirror(b):
             if b in SMIR:
                 spare = stage.tile([P, PACK, P], BF16, name="spare", bufs=1)
                 nc.scalar.activation(out=spare[:], in_=mirrored[b][:], func=ACT.Copy, accum_out=row_sums[:, b, 0:1])
@@ -203,34 +212,48 @@ def tile_dynamicgraphspatialconv_pb_kernel(tc, x, adj_param, tx1, cheb01, w_cheb
                     op=ALU.add,
                 )
 
-        bias_turned = banks.tile([P, P], BF16, tag="bank")
-        nc.tensor.transpose(out=bias_turned[:], in_=bias_rows[:], identity=ident_b[:])
-
         deg2 = const.tile([P, ROWS], F32)
-        nc.vector.tensor_reduce(out=deg2[:], in_=row_sums[:], axis=mybir.AxisListType.X, op=ALU.add)
         root = const.tile([P, 2, ROWS], F32)
-        for i, scale in enumerate((-1.0, -0.25)):
-            nc.scalar.activation(out=root[:, i, :], in_=deg2[:], func=ACT.Sqrt, scale=scale)
         rnorm = const.tile([P, 2, ROWS], F32)
-        nc.vector.reciprocal(out=rnorm[:], in_=root[:])
+
+        def sum_rows(half):
+            chunks = slice(half * PACK, (half + 1) * PACK)
+            nc.vector.tensor_reduce(
+                out=deg2[:, chunks], in_=row_sums[:, chunks, :], axis=mybir.AxisListType.X, op=ALU.add
+            )
+            for i, scale in enumerate((-1.0, -0.25)):
+                nc.scalar.activation(out=root[:, i, chunks], in_=deg2[:, chunks], func=ACT.Sqrt, scale=scale)
+
+        factor = {}
+
+        def invert_roots(half):
+            chunks = slice(half * PACK, (half + 1) * PACK)
+            nc.vector.reciprocal(out=rnorm[:, :, chunks], in_=root[:, :, chunks])
+            if half == 0:
+                factor[half] = banks.tile([P, PACK, P], F32, tag="bank", name="factor")
+            else:
+                factor[half] = factors.tile([P, PACK, P], F32, tag="mirrored", name="factor")
+            for i in range(PACK):
+                r = half * PACK + i
+                nc.tensor.transpose(
+                    out=factor[half][:, i, :], in_=rnorm[:, 1, r : r + 1].to_broadcast([P, P]), identity=ident_f[:]
+                )
 
         w_codes = const.tile([P, C_OUT], U32, align_bytes=64)
         w_scales = const.tile([P, C_OUT], U8, align_bytes=64)
         bias_col = const.tile([P, 1], F32)
-        nc.vector.tensor_copy(out=bias_col[:], in_=bias_turned[:, 0:1])
 
         def quantise_w():
             nc.vector.quantize_mx(
                 out=w_codes[:].bitcast(FP8X4), scales=w_scales[:], in_=w_grouped[:].rearrange("p o m -> p (o m)")
             )
 
-        factor = [factors.tile([P, PACK, P], F32, tag="mirrored", name="factor") for i in range(HALVES)]
-        for half in (1, 0):
-            for i in range(PACK):
-                r = half * PACK + i
-                nc.tensor.transpose(
-                    out=factor[half][:, i, :], in_=rnorm[:, 1, r : r + 1].to_broadcast([P, P]), identity=ident_f[:]
-                )
+        def regroup_on_vector(t, g, half):
+            cols = slice(half * C_IN // 2, (half + 1) * C_IN // 2)
+            nc.vector.tensor_copy(
+                out=tx1_grouped[t][:, g, cols, :],
+                in_=tx1_raw[:, t, g * PACK : (g + 1) * PACK, cols].rearrange("p j c -> p c j"),
+            )
 
         s_codes = keep.tile([P, PAIRS, PASSES, 2 * P], U32, align_bytes=64)
         s_scales = keep.tile([P, PAIRS, PASSES, 2 * P], U8, align_bytes=64)
@@ -375,38 +398,48 @@ def tile_dynamicgraphspatialconv_pb_kernel(tc, x, adj_param, tx1, cheb01, w_cheb
             regroup_on_scalar(t, g, 1)
 
         last = STEPS - 1
-        units = [(0, 0), (0, 1), (1, 0), (0, 2), (1, 1), (2, 0), (2, 1), (0, 3), (1, 2), (2, 2), (1, 3), (2, 3)]
+        units = [(0, 0), (0, 1), (0, 2), (1, 0), (1, 1), (2, 0), (2, 1), (0, 3), (1, 2), (2, 2), (1, 3), (2, 3)]
 
-        quantise_tx1(0, 0)
-        quantise_tx1(0, 1)
+        sum_rows(0)
+        invert_roots(0)
+        scale_rows(0, 0)
+        for b in bottom:
+            sum_mirror(b)
+        bias_turned = results.tile([P, P], BF16, tag="mirrored", name="bias_turned")
+        nc.tensor.transpose(out=bias_turned[:], in_=bias_rows[:], identity=ident_b[:])
+        scale_rows(1, 0)
+        sum_rows(1)
+        scale_columns(0, 0)
+        invert_roots(1)
+        nc.vector.tensor_copy(out=bias_col[:], in_=bias_turned[:, 0:1])
         scale_rows(2, 0)
         scale_rows(3, 0)
-        scale_rows(0, 0)
-        scale_rows(1, 0)
+        scale_columns(1, 0)
         scale_columns(2, 0)
         scale_columns(3, 0)
+        scale_rows(2, 1)
+        scale_rows(3, 1)
         mirror_s(0)
         mirror_s(1)
-        scale_columns(0, 0)
-        scale_columns(1, 0)
+        quantise_tx1(0)
+        scale_columns(2, 1)
         quantise_s(0)
         first_product(0, 0)
         first_product(0, 1)
         regroup_twice(1, 0)
-        scale_rows(2, 1)
         regroup_twice(1, 1)
-        scale_rows(3, 1)
         regroup_twice(2, 0)
         regroup_twice(2, 1)
-        quantise_w()
         quantise_s(1)
         first_product(0, 2)
         first_product(0, 3)
+        quantise_w()
+        scale_columns(3, 1)
+        quantise_s(2)
         plan = {
-            (0, 0): lambda: (scale_columns(2, 1), quantise_tx1(1, 0)),
-            (0, 1): lambda: (quantise_tx1(1, 1), quantise_s(2), scale_columns(3, 1)),
-            (1, 0): lambda: (quantise_s(3), turn_cheb(0)),
-            (0, 2): lambda: (quantise_tx1(2, 0), quantise_tx1(2, 1)),
+            (0, 1): lambda: quantise_tx1(1),
+            (0, 2): lambda: (quantise_s(3), turn_cheb(0)),
+            (1, 0): lambda: quantise_tx1(2),
             (1, 1): lambda: turn_cheb(2),
             (2, 1): lambda: turn_cheb(4),
             (2, 2): lambda: turn_cheb(6),

@@ -189,7 +189,6 @@ def tile_dynamicgraphspatialconv_pb_kernel(tc, x, adj_param, tx1, cheb01, w_cheb
         table_warm = const.tile([P, 1], F32)
         nc.scalar.activation(out=table_warm[:], in_=sig[:, PACK - 1, NODES - 1 : NODES], func=ACT.Sqrt)
         w_grouped = const.tile([P, C_OUT, PACK], BF16, align_bytes=64)
-        nc.scalar.copy(out=grouped_view(w_grouped[:]), in_=rows_view(w_raw[:]))
         for tg in GREG:
             regroup_on_gpsimd(*tg)
         mirrored = {b: (results if b < 6 else factors).tile([P, PACK, P], F32, tag="mirrored", name="mirrored") for b in bottom}
@@ -213,22 +212,21 @@ def tile_dynamicgraphspatialconv_pb_kernel(tc, x, adj_param, tx1, cheb01, w_cheb
                 )
 
         deg2 = const.tile([P, ROWS], F32)
-        root = const.tile([P, 2, ROWS], F32)
-        rnorm = const.tile([P, 2, ROWS], F32)
+        root = const.tile([P, ROWS], F32)
+        rnorm = const.tile([P, ROWS], F32)
 
         def sum_rows(half):
             chunks = slice(half * PACK, (half + 1) * PACK)
             nc.vector.tensor_reduce(
                 out=deg2[:, chunks], in_=row_sums[:, chunks, :], axis=mybir.AxisListType.X, op=ALU.add
             )
-            for i, scale in enumerate((-1.0, -0.25)):
-                nc.scalar.activation(out=root[:, i, chunks], in_=deg2[:, chunks], func=ACT.Sqrt, scale=scale)
+            nc.scalar.activation(out=root[:, chunks], in_=deg2[:, chunks], func=ACT.Sqrt, scale=-0.5)
 
         factor = {}
 
         def invert_roots(half):
             chunks = slice(half * PACK, (half + 1) * PACK)
-            nc.vector.reciprocal(out=rnorm[:, :, chunks], in_=root[:, :, chunks])
+            nc.vector.reciprocal(out=rnorm[:, chunks], in_=root[:, chunks])
             if half == 0:
                 factor[half] = banks.tile([P, PACK, P], F32, tag="bank", name="factor")
             else:
@@ -236,12 +234,15 @@ def tile_dynamicgraphspatialconv_pb_kernel(tc, x, adj_param, tx1, cheb01, w_cheb
             for i in range(PACK):
                 r = half * PACK + i
                 nc.tensor.transpose(
-                    out=factor[half][:, i, :], in_=rnorm[:, 1, r : r + 1].to_broadcast([P, P]), identity=ident_f[:]
+                    out=factor[half][:, i, :], in_=rnorm[:, r : r + 1].to_broadcast([P, P]), identity=ident_f[:]
                 )
 
         w_codes = const.tile([P, C_OUT], U32, align_bytes=64)
         w_scales = const.tile([P, C_OUT], U8, align_bytes=64)
         bias_col = const.tile([P, 1], F32)
+
+        def group_w():
+            nc.scalar.copy(out=grouped_view(w_grouped[:]), in_=rows_view(w_raw[:]))
 
         def quantise_w():
             nc.vector.quantize_mx(
@@ -283,7 +284,7 @@ def tile_dynamicgraphspatialconv_pb_kernel(tc, x, adj_param, tx1, cheb01, w_cheb
                     out=scaled[(q, g)][:, j, :],
                     in_=both[:, b, 2 * q * P : 2 * (q + 1) * P],
                     func=ACT.Copy,
-                    scale=rnorm[:, 0, b : b + 1],
+                    scale=rnorm[:, b : b + 1],
                 )
 
         def scale_columns(q, g):
@@ -421,6 +422,7 @@ def tile_dynamicgraphspatialconv_pb_kernel(tc, x, adj_param, tx1, cheb01, w_cheb
         scale_rows(3, 1)
         mirror_s(0)
         mirror_s(1)
+        group_w()
         quantise_tx1(0)
         scale_columns(2, 1)
         quantise_s(0)

@@ -24,7 +24,6 @@ HALVES = NODES // HALF
 PAIRS = NODES // (2 * P)
 TILES = NODES // P
 RUN = 4
-SMIR = (7,)
 GREG = ((0, 0), (0, 1))
 GP = 1
 PAIR = 2
@@ -191,25 +190,24 @@ def tile_dynamicgraphspatialconv_pb_kernel(tc, x, adj_param, tx1, cheb01, w_cheb
         w_grouped = const.tile([P, C_OUT, PACK], BF16, align_bytes=64)
         for tg in GREG:
             regroup_on_gpsimd(*tg)
-        mirrored = {b: (results if b < 6 else factors).tile([P, PACK, P], F32, tag="mirrored", name="mirrored") for b in bottom}
+        mirrored = {b: (results if b < 6 else factors).tile([P, P], F32, tag="mirrored", name="mirrored") for b in bottom}
         for i in top:
             symmetrise(i, 4, 4)
         for i in top:
             for b in bottom:
-                nc.tensor.transpose(
-                    out=mirrored[b][:, i, :], in_=both[:, i, b * P : (b + 1) * P], identity=ident_f[:]
+                nc.tensor.matmul(
+                    out=mirrored[b][:],
+                    lhsT=both[:, i, b * P : (b + 1) * P],
+                    rhs=ident_f[:],
+                    is_transpose=True,
+                    start=(i == 0),
+                    stop=(i == PACK - 1),
                 )
+
         def sum_mirror(b):
-            if b in SMIR:
-                spare = stage.tile([P, PACK, P], BF16, name="spare", bufs=1)
-                nc.scalar.activation(out=spare[:], in_=mirrored[b][:], func=ACT.Copy, accum_out=row_sums[:, b, 0:1])
-            else:
-                nc.vector.tensor_reduce(
-                    out=row_sums[:, b, 0:1],
-                    in_=mirrored[b][:].rearrange("p i w -> p (i w)"),
-                    axis=mybir.AxisListType.X,
-                    op=ALU.add,
-                )
+            nc.vector.tensor_reduce(
+                out=row_sums[:, b, 0:1], in_=mirrored[b][:], axis=mybir.AxisListType.X, op=ALU.add
+            )
 
         deg2 = const.tile([P, ROWS], F32)
         root = const.tile([P, ROWS], F32)
@@ -408,8 +406,8 @@ def tile_dynamicgraphspatialconv_pb_kernel(tc, x, adj_param, tx1, cheb01, w_cheb
             sum_mirror(b)
         bias_turned = results.tile([P, P], BF16, tag="mirrored", name="bias_turned")
         nc.tensor.transpose(out=bias_turned[:], in_=bias_rows[:], identity=ident_b[:])
-        scale_rows(1, 0)
         sum_rows(1)
+        scale_rows(1, 0)
         scale_columns(0, 0)
         invert_roots(1)
         nc.vector.tensor_copy(out=bias_col[:], in_=bias_turned[:, 0:1])
@@ -423,8 +421,8 @@ def tile_dynamicgraphspatialconv_pb_kernel(tc, x, adj_param, tx1, cheb01, w_cheb
         mirror_s(0)
         mirror_s(1)
         group_w()
-        quantise_tx1(0)
         scale_columns(2, 1)
+        quantise_tx1(0)
         quantise_s(0)
         first_product(0, 0)
         first_product(0, 1)

from contextlib import ExitStack

import concourse.mybir as mybir
from concourse.masks import make_identity

F32 = mybir.dt.float32
BF16 = mybir.dt.bfloat16
U32 = mybir.dt.uint32
U8 = mybir.dt.uint8
FP8X4 = mybir.dt.float8_e4m3fn_x4
ALU = mybir.AluOpType
ACT = mybir.ActivationFunctionType

P = 128
PACK = 4
NODES = 1024
C_IN = 512
C_OUT = 128
STEPS = 3
ROWS = NODES // P
PASSES = NODES // (P * PACK)
HALF = 512
HALVES = NODES // HALF
PAIRS = NODES // (2 * P)
TILES = NODES // P
RUN = 4
GREG = ((0, 0), (0, 1))
GP = 1
PAIR = 2
VFIN = 2
QUARTERS = 4

FLOPS = 2 * STEPS * NODES * NODES * C_IN + 2 * STEPS * NODES * C_IN * C_OUT


def grouped_view(dst, run=RUN):
    return dst.rearrange("p (c i) j -> p c j i", i=run)


def rows_view(src, run=RUN):
    return src.rearrange("p j (c i) -> p c j i", i=run)


def tile_dynamicgraphspatialconv_pb_kernel(tc, x, adj_param, tx1, cheb01, w_cheb2, cheb_bias, out):
    nc = tc.nc
    with ExitStack() as ctx:
        ctx.enter_context(tc.manual_schedule())
        const = ctx.enter_context(tc.tile_pool(name="const", bufs=1))
        keep = ctx.enter_context(tc.tile_pool(name="keep", bufs=1))
        stage = ctx.enter_context(tc.tile_pool(name="stage", bufs=3))
        leave = ctx.enter_context(tc.tile_pool(name="leave", bufs=8))
        shared = ctx.enter_context(tc.tile_pool(name="shared", bufs=1))
        early = ctx.enter_context(tc.tile_pool(name="early", bufs=2))
        banks = ctx.enter_context(tc.psum_pool(name="banks", bufs=4))
        results = ctx.enter_context(tc.psum_pool(name="results", bufs=2))
        factors = ctx.enter_context(tc.psum_pool(name="factors", bufs=2))

        bias_rows = const.tile([P, P], BF16)
        nc.vector.memset(bias_rows[:], 0.0)

        param = shared.tile([P, ROWS, NODES], BF16, tag="param", align_bytes=64)
        param_rows = adj_param.rearrange("(b p) v -> p b v", p=P)

        def load_param(chunks, first, end):
            cols = slice(first * P, end * P)
            nc.sync.dma_start(out=param[:, chunks, cols], in_=param_rows[:, chunks, cols])

        load_param(slice(0, 2), 0, 2)
        load_param(slice(0, 2), 2, 4)
        load_param(slice(2, 4), 0, 4)
        load_param(slice(4, 6), 4, 8)
        load_param(slice(6, 8), 4, 8)
        load_param(slice(4, 8), 0, 4)
        load_param(slice(0, 4), 4, 8)
        tx1_raw = keep.tile([P, STEPS, ROWS, C_IN], BF16)

        def load_tx1(t):
            nc.sync.dma_start(out=tx1_raw[:, t], in_=tx1[0, t].rearrange("(b p) c -> p b c", p=P))

        x_sb = keep.tile([P, PACK, NODES * STEPS], BF16)
        x_rows = x[0].rearrange("(m p) v t -> p m (v t)", p=P)

        def load_x(first, end):
            cols = slice(first * STEPS, end * STEPS)
            nc.sync.dma_start(out=x_sb[:, :, cols], in_=x_rows[:, :, cols])

        load_tx1(0)
        w_raw = const.tile([P, PACK, C_OUT], BF16)
        nc.sync.dma_start(out=w_raw[:], in_=w_cheb2.rearrange("(m p) o -> p m o", p=P))
        nc.sync.dma_start(out=bias_rows[0:1, :], in_=cheb_bias.rearrange("(r o) -> r o", r=1))
        load_x(0, 256)
        load_tx1(1)
        load_tx1(2)
        load_x(256, 512)
        load_x(512, NODES)
        cheb_raw = keep.tile([P, STEPS, ROWS, C_OUT], BF16)
        for t in range(STEPS):
            nc.sync.dma_start(out=cheb_raw[:, t], in_=cheb01[0, t].rearrange("(b p) o -> p b o", p=P))

        ident_f = const.tile([P, P], F32)
        make_identity(nc, ident_f[:])
        ident_b = const.tile([P, P], BF16)
        make_identity(nc, ident_b[:])
        off_diag = const.tile([P, P], F32)
        nc.vector.tensor_scalar(
            out=off_diag[:], in0=ident_f[:], scalar1=-1.0, scalar2=1.0, op0=ALU.mult, op1=ALU.add
        )

        sig = shared.tile([P, ROWS, NODES], F32, tag="sig", align_bytes=64)
        both = keep.tile([P, ROWS, NODES], F32)
        row_sums = const.tile([P, ROWS, QUARTERS], F32)
        nc.vector.memset(row_sums[:], 0.0)

        def sigmoid_piece(b, first, count):
            cols = slice(first * P, (first + count) * P)
            nc.scalar.activation(out=sig[:, b, cols], in_=param[:, b, cols], func=ACT.Sigmoid)
            if first <= b < first + count:
                diag = slice(b * P, (b + 1) * P)
                nc.gpsimd.tensor_tensor(out=sig[:, b, diag], in0=sig[:, b, diag], in1=off_diag[:], op=ALU.mult)

        def symmetrise(b, first, count):
            cols = slice(first * P, (first + count) * P)
            turned = banks.tile([P, PACK, P], F32, tag="bank")
            for i in range(count):
                nc.tensor.transpose(
                    out=turned[:, i, :], in_=sig[:, first + i, b * P : (b + 1) * P], identity=ident_f[:]
                )
            slot = first * QUARTERS // ROWS
            nc.vector.scalar_tensor_tensor(
                out=both[:, b, cols],
                in0=turned[:, 0:count, :].rearrange("p i w -> p (i w)"),
                scalar=-1.0,
                in1=sig[:, b, cols],
                op0=ALU.mult,
                op1=ALU.subtract,
                accum_out=row_sums[:, b, slot : slot + 1],
            )

        tx1_codes = keep.tile([P, STEPS, PASSES, C_IN], U32, align_bytes=64)
        tx1_scales = keep.tile([P, STEPS, PASSES, C_IN], U8, align_bytes=64)
        tx1_grouped = {}

        def regroup_views(t, g, first, end):
            if t not in tx1_grouped:
                tx1_grouped[t] = early.tile([P, PASSES, C_IN, PACK], BF16, align_bytes=64, name="tx1_grouped")
            return (
                grouped_view(tx1_grouped[t][:, g, first:end, :]),
                rows_view(tx1_raw[:, t, g * PACK : (g + 1) * PACK, first:end]),
            )

        def regroup_on_gpsimd(t, g):
            for i in range(GP):
                dst, rows = regroup_views(t, g, i * C_IN // GP, (i + 1) * C_IN // GP)
                nc.gpsimd.tensor_scalar(out=dst, in0=rows, scalar1=1.0, scalar2=0.0, op0=ALU.mult, op1=ALU.add)

        def regroup_on_scalar(t, g, half):
            dst, rows = regroup_views(t, g, half * C_IN // 2, (half + 1) * C_IN // 2)
            nc.scalar.copy(out=dst, in_=rows)

        def quantise_tx1(t):
            nc.vector.quantize_mx(
                out=tx1_codes[:, t].rearrange("p g c -> p (g c)").bitcast(FP8X4),
                scales=tx1_scales[:, t].rearrange("p g c -> p (g c)"),
                in_=tx1_grouped[t][:].rearrange("p g c j -> p (g c j)"),
            )

        top = range(0, PACK)
        bottom = range(PACK, ROWS)
        for first in (0, 2):
            for b in (0, 1):
                sigmoid_piece(b, first, 2)
        for b in (2, 3):
            sigmoid_piece(b, 0, 4)
        for b in (0, 1):
            symmetrise(b, 0, 2)
        for b in (2, 3):
            symmetrise(b, 0, 4)
        for b in (0, 1):
            symmetrise(b, 2, 2)
        for b in bottom:
            sigmoid_piece(b, 4, 4)
        for b in bottom:
            symmetrise(b, 4, 4)
        for b in bottom:
            sigmoid_piece(b, 0, 4)
        for b in top:
            sigmoid_piece(b, 4, 4)
        table_warm = const.tile([P, 1], F32)
        nc.scalar.activation(out=table_warm[:], in_=sig[:, PACK - 1, NODES - 1 : NODES], func=ACT.Sqrt)
        w_grouped = const.tile([P, C_OUT, PACK], BF16, align_bytes=64)
        for tg in GREG:
            regroup_on_gpsimd(*tg)
        mirrored = {b: (results if b < 6 else factors).tile([P, P], F32, tag="mirrored", name="mirrored") for b in bottom}
        for i in top:
            symmetrise(i, 4, 4)
        for i in top:
            for b in bottom:
                nc.tensor.matmul(
                    out=mirrored[b][:],
                    lhsT=both[:, i, b * P : (b + 1) * P],
                    rhs=ident_f[:],
                    is_transpose=True,
                    start=(i == 0),
                    stop=(i == PACK - 1),
                )

        def sum_mirror(b):
            nc.vector.tensor_reduce(
                out=row_sums[:, b, 0:1], in_=mirrored[b][:], axis=mybir.AxisListType.X, op=ALU.add
            )

        deg2 = const.tile([P, ROWS], F32)
        root = const.tile([P, ROWS], F32)
        rnorm = const.tile([P, ROWS], F32)

        def sum_rows(half):
            chunks = slice(half * PACK, (half + 1) * PACK)
            nc.vector.tensor_reduce(
                out=deg2[:, chunks], in_=row_sums[:, chunks, :], axis=mybir.AxisListType.X, op=ALU.add
            )
            nc.scalar.activation(out=root[:, chunks], in_=deg2[:, chunks], func=ACT.Sqrt, scale=-0.5)

        factor = {}

        def invert_roots(half):
            chunks = slice(half * PACK, (half + 1) * PACK)
            nc.vector.reciprocal(out=rnorm[:, chunks], in_=root[:, chunks])
            if half == 0:
                factor[half] = banks.tile([P, PACK, P], F32, tag="bank", name="factor")
            else:
                factor[half] = factors.tile([P, PACK, P], F32, tag="mirrored", name="factor")
            for i in range(PACK):
                r = half * PACK + i
                nc.tensor.transpose(
                    out=factor[half][:, i, :], in_=rnorm[:, r : r + 1].to_broadcast([P, P]), identity=ident_f[:]
                )

        w_codes = const.tile([P, C_OUT], U32, align_bytes=64)
        w_scales = const.tile([P, C_OUT], U8, align_bytes=64)
        bias_col = const.tile([P, 1], F32)

        def group_w():
            nc.scalar.copy(out=grouped_view(w_grouped[:]), in_=rows_view(w_raw[:]))

        def quantise_w():
            nc.vector.quantize_mx(
                out=w_codes[:].bitcast(FP8X4), scales=w_scales[:], in_=w_grouped[:].rearrange("p o m -> p (o m)")
            )

        def regroup_on_vector(t, g, half):
            cols = slice(half * C_IN // 2, (half + 1) * C_IN // 2)
            nc.vector.tensor_copy(
                out=tx1_grouped[t][:, g, cols, :],
                in_=tx1_raw[:, t, g * PACK : (g + 1) * PACK, cols].rearrange("p j c -> p c j"),
            )

        s_codes = keep.tile([P, PAIRS, PASSES, 2 * P], U32, align_bytes=64)
        s_scales = keep.tile([P, PAIRS, PASSES, 2 * P], U8, align_bytes=64)
        tx2_codes = shared.tile([P, STEPS, NODES], U32, tag="param", name="tx2_codes", align_bytes=64)
        tx2_scales = keep.tile([P, STEPS, NODES], U8, align_bytes=64)
        s_grouped = shared.tile([P, PAIRS, PASSES, 2 * P, PACK], BF16, tag="sig", name="s_grouped", align_bytes=64)
        cheb_t = keep.tile([P, NODES, STEPS], BF16)
        scaled = {}
        acc = {}
        tx2_grouped = {}

        def turn_cheb(r):
            turned = banks.tile([P, 2, STEPS, P], BF16, tag="bank", name="cheb_turned")
            for i in range(2):
                for t in range(STEPS):
                    nc.tensor.transpose(out=turned[:, i, t, :], in_=cheb_raw[:, t, r + i, :], identity=ident_b[:])
            for i in range(2):
                nc.scalar.copy(
                    out=cheb_t[:, (r + i) * P : (r + i + 1) * P, :], in_=turned[:, i].rearrange("p t v -> p v t")
                )

        def scale_rows(q, g):
            scaled[(q, g)] = stage.tile([P, PACK, 2 * P], F32, name="scaled", bufs=4)
            for j in range(PACK):
                b = g * PACK + j
                nc.scalar.activation(
                    out=scaled[(q, g)][:, j, :],
                    in_=both[:, b, 2 * q * P : 2 * (q + 1) * P],
                    func=ACT.Copy,
                    scale=rnorm[:, b : b + 1],
                )

        def scale_columns(q, g):
            columns = factor[q // 2][:].rearrange("p i v -> p (i v)")[:, (q % 2) * 2 * P : (q % 2 + 1) * 2 * P]
            nc.vector.tensor_tensor(
                out=grouped_view(s_grouped[:, q, g], PAIR),
                in0=rows_view(scaled[(q, g)][:], PAIR),
                in1=columns.rearrange("p (c i) -> p c i", i=PAIR)
                .unsqueeze(2)
                .to_broadcast([P, 2 * P // PAIR, PACK, PAIR]),
                op=ALU.mult,
            )

        def mirror_s(q):
            turned = banks.tile([P, 2, PACK, P], BF16, tag="bank", name="s_turned")
            for i in range(2):
                for j in range(PACK):
                    r = PACK + j
                    nc.tensor.transpose(
                        out=turned[:, i, j, :],
                        in_=s_grouped[:, r // 2, 0, (r % 2) * P : (r % 2 + 1) * P, 2 * q + i],
                        identity=ident_b[:],
                    )
            for i in range(2):
                nc.scalar.copy(
                    out=s_grouped[:, q, 1, i * P : (i + 1) * P, :], in_=turned[:, i].rearrange("p j v -> p v j")
                )

        def quantise_s(q):
            nc.vector.quantize_mx(
                out=s_codes[:, q].rearrange("p g v -> p (g v)").bitcast(FP8X4),
                scales=s_scales[:, q].rearrange("p g v -> p (g v)"),
                in_=s_grouped[:, q].rearrange("p g v j -> p (g v j)"),
            )

        def first_product(t, r):
            acc[(t, r)] = banks.tile([P, PACK, P], F32, tag="bank", name="acc")
            for m in range(PACK):
                for g in range(PASSES):
                    nc.tensor.matmul_mx(
                        out=acc[(t, r)][:, m, :],
                        lhsT=tx1_codes[:, t, g, m * P : (m + 1) * P].bitcast(FP8X4),
                        lhsT_scale=tx1_scales[:, t, g, m * P : (m + 1) * P],
                        rhs=s_codes[:, r // 2, g, (r % 2) * P : (r % 2 + 1) * P].bitcast(FP8X4),
                        rhs_scale=s_scales[:, r // 2, g, (r % 2) * P : (r % 2 + 1) * P],
                        start=(g == 0),
                        stop=(g == PASSES - 1),
                    )

        def subtract_x(t, r):
            if r % 2 == 0:
                tx2_grouped[(t, r // 2)] = stage.tile([P, 2 * P, PACK], BF16, align_bytes=64, name="tx2_grouped")
            grouped = tx2_grouped[(t, r // 2)][:, (r % 2) * P : (r % 2 + 1) * P, :]
            x_tile = x_sb[:, :, r * P * STEPS : (r + 1) * P * STEPS].rearrange("p m (v t) -> p m v t", t=STEPS)
            nc.vector.tensor_tensor(
                out=grouped_view(grouped),
                in0=rows_view(acc[(t, r)][:]),
                in1=rows_view(x_tile[:, :, :, t]),
                op=ALU.subtract,
            )

        def quantise_tx2(t, first, count):
            nodes = slice(first * P, (first + count) * P)
            part = slice((first % 2) * P, (first % 2 + count) * P)
            nc.vector.quantize_mx(
                out=tx2_codes[:, t, nodes].bitcast(FP8X4),
                scales=tx2_scales[:, t, nodes],
                in_=tx2_grouped[(t, first // 2)][:, part, :].rearrange("p v m -> p (v m)"),
            )

        def finish(r):
            nodes = slice(r * P, (r + 1) * P)
            mixed = results.tile([P, STEPS, P], F32, tag="mirrored", name="mixed")
            for u in range(STEPS):
                nc.tensor.matmul_mx(
                    out=mixed[:, u, :],
                    lhsT=w_codes[:].bitcast(FP8X4),
                    lhsT_scale=w_scales[:],
                    rhs=tx2_codes[:, u, nodes].bitcast(FP8X4),
                    rhs_scale=tx2_scales[:, u, nodes],
                    start=True,
                    stop=True,
                )
            answer = leave.tile([P, P, STEPS], F32)
            if r >= TILES - VFIN:
                nc.vector.scalar_tensor_tensor(
                    out=answer[:],
                    in0=mixed[:].rearrange("p u v -> p v u"),
                    scalar=bias_col[:, 0:1],
                    in1=cheb_t[:, nodes, :],
                    op0=ALU.add,
                    op1=ALU.add,
                )
                nc.sync.dma_start(out=out[0, :, nodes, :], in_=answer[:])
                return
            biased = leave.tile([P, P, STEPS], F32, bufs=2)
            nc.scalar.activation(
                out=biased[:], in_=mixed[:].rearrange("p u v -> p v u"), func=ACT.Identity, bias=bias_col[:, 0:1]
            )
            for h in range(2):
                part = slice(h * P // 2, (h + 1) * P // 2)
                nc.gpsimd.tensor_tensor(
                    out=answer[:, part, :],
                    in0=biased[:, part, :],
                    in1=cheb_t[:, r * P + h * P // 2 : r * P + (h + 1) * P // 2, :],
                    op=ALU.add,
                )
            nc.sync.dma_start(out=out[0, :, nodes, :], in_=answer[:])

        def regroup_twice(t, g):
            regroup_on_scalar(t, g, 0)
            regroup_on_scalar(t, g, 1)

        last = STEPS - 1
        units = [(0, 0), (0, 1), (0, 2), (1, 0), (1, 1), (2, 0), (2, 1), (0, 3), (1, 2), (2, 2), (1, 3), (2, 3)]

        sum_rows(0)
        invert_roots(0)
        scale_rows(0, 0)
        for b in bottom:
            sum_mirror(b)
        bias_turned = results.tile([P, P], BF16, tag="mirrored", name="bias_turned")
        nc.tensor.transpose(out=bias_turned[:], in_=bias_rows[:], identity=ident_b[:])
        sum_rows(1)
        scale_rows(1, 0)
        scale_columns(0, 0)
        invert_roots(1)
        nc.vector.tensor_copy(out=bias_col[:], in_=bias_turned[:, 0:1])
        scale_rows(2, 0)
        scale_rows(3, 0)
        scale_columns(1, 0)
        scale_columns(2, 0)
        scale_columns(3, 0)
        scale_rows(2, 1)
        scale_rows(3, 1)
        mirror_s(0)
        mirror_s(1)
        group_w()
        scale_columns(2, 1)
        quantise_tx1(0)
        quantise_s(0)
        first_product(0, 0)
        first_product(0, 1)
        regroup_twice(1, 0)
        regroup_twice(1, 1)
        regroup_twice(2, 0)
        regroup_twice(2, 1)
        quantise_s(1)
        first_product(0, 2)
        first_product(0, 3)
        quantise_w()
        scale_columns(3, 1)
        quantise_s(2)
        plan = {
            (0, 1): lambda: quantise_tx1(1),
            (0, 2): lambda: (quantise_s(3), turn_cheb(0)),
            (1, 0): lambda: quantise_tx1(2),
            (1, 1): lambda: turn_cheb(2),
            (2, 1): lambda: turn_cheb(4),
            (2, 2): lambda: turn_cheb(6),
        }
        waiting = None
        for n, (t, q) in enumerate(units):
            subtract_x(t, 2 * q)
            if waiting:
                quantise_tx2(waiting[0], 2 * waiting[1], 2)
            subtract_x(t, 2 * q + 1)
            plan.get((t, q), lambda: 0)()
            if 1 <= n < len(units) - 1:
                ahead = units[n + 1]
                first_product(ahead[0], 2 * ahead[1])
                first_product(ahead[0], 2 * ahead[1] + 1)
            if waiting and waiting[0] == last:
                finish(2 * waiting[1])
                finish(2 * waiting[1] + 1)
            waiting = (t, q)
        for r in (TILES - 2, TILES - 1):
            quantise_tx2(last, r, 1)
        for r in (TILES - 2, TILES - 1):
            finish(r)
